import numpy as np
import ml_dtypes


def mxq(x, axis, fmt="e4m3"):
    dtype, down = {"e4m3": (ml_dtypes.float8_e4m3fn, 7), "e5m2": (ml_dtypes.float8_e5m2, 14)}[fmt]
    v = np.moveaxis(np.asarray(x, np.float32).astype(ml_dtypes.bfloat16).astype(np.float64), axis, -1)
    blocks = v.reshape(v.shape[:-1] + (-1, 32))
    amax = np.abs(blocks).max(-1, keepdims=True)
    byte = np.maximum(np.where(amax > 0, np.frexp(amax)[1] - 1 + 127, 0) - down, 1)
    scale = np.exp2(byte - 127.0)
    codes = (blocks / scale).astype(np.float32).astype(dtype).astype(np.float64)
    return np.moveaxis((codes * scale).reshape(v.shape), -1, axis)


WIDE = False


def mx_kscale(k):
    if not WIDE:
        return np.ones(k)
    levels = np.array([10, -10, 5, -5, 0])
    if k % 512:
        return np.exp2(np.random.permutation(np.resize(levels, k // 32))).repeat(32)
    a = np.empty((k // 512, 16))
    for p in range(k // 512):
        a[p, :8] = np.random.permutation(np.resize(levels, 8))
        for g in range(8):
            far = levels[np.abs(levels - a[p, g]) >= 10]
            a[p, g + 8] = far[np.random.randint(len(far))]
    return np.exp2(a.ravel()).repeat(32)


BF16 = ml_dtypes.bfloat16


def bf(x):
    return np.asarray(x, np.float32).astype(BF16)


def f64(x):
    return np.asarray(x).astype(np.float64)


B, C, CK, CV, CO, H, W, P1, P2, P3, P4 = 1, 1024, 256, 256, 1024, 24, 48, 1, 3, 6, 8
PSP_SIZES = (P1, P2, P3, P4)
EPS = 1e-5
N = H * W


def bnrelu(x, gamma, beta, mean, var):
    inv = 1.0 / np.sqrt(var + EPS)
    return np.maximum((x - mean[None, :, None]) * (inv * gamma)[None, :, None] + beta[None, :, None], 0.0)


def psp(x):
    b, c = x.shape[:2]
    outs = []
    for s in PSP_SIZES:
        outs.append(x.reshape(b, c, s, H // s, s, W // s).mean(axis=(3, 5)).reshape(b, c, s * s))
    return np.concatenate(outs, axis=-1)


def setup_inputs():
    s = mx_kscale(C)
    fine = np.random.standard_normal((B, C, H, W))
    coarse = np.random.standard_normal((B, C, P4, P4))
    coarse = np.repeat(np.repeat(coarse, H // P4, axis=2), W // P4, axis=3)
    return {"feats": bf((fine + coarse) * np.sqrt(0.5) * s[None, :, None, None]),
            "Wk": bf(np.random.standard_normal((CK, C)) * 1.5 / np.sqrt(C) / s[None, :]),
            "bk": bf(np.random.standard_normal(CK) * 0.2),
            "gk": bf(1.0 + 0.1 * np.random.standard_normal(CK)),
            "betak": bf(np.random.standard_normal(CK) * 0.2),
            "mk": bf(np.random.standard_normal(CK) * 0.2),
            "vk": bf(np.random.uniform(0.5, 1.5, CK)),
            "Wv": bf(np.random.standard_normal((CV, C)) / np.sqrt(C) / s[None, :]),
            "bv": bf(np.random.standard_normal(CV) * 0.2)}


def reference(feats, Wk, bk, gk, betak, mk, vk, Wv, bv):
    xq = mxq(f64(feats).reshape(B, C, N), 1, "e4m3")
    pre = (mxq(f64(Wk), 1, "e4m3") @ xq) + f64(bk)[None, :, None]
    kf = bnrelu(pre, f64(gk), f64(betak), f64(mk), f64(vk)).reshape(B, CK, H, W)
    keyp = psp(kf)
    val = ((mxq(f64(Wv), 1, "e4m3") @ xq) + f64(bv)[None, :, None]).reshape(B, CV, H, W)
    value = psp(val).transpose(0, 2, 1)
    return kf, keyp, value

@@ -1,0 +1,354 @@
+from contextlib import ExitStack
+
+import concourse.mybir as mybir
+from concourse.masks import make_identity
+
+F32 = mybir.dt.float32
+BF16 = mybir.dt.bfloat16
+I32 = mybir.dt.int32
+U32 = mybir.dt.uint32
+U8 = mybir.dt.uint8
+FP8X4 = mybir.dt.float8_e4m3fn_x4
+ALU = mybir.AluOpType
+ACT = mybir.ActivationFunctionType
+AXIS = mybir.AxisListType
+
+P = 128
+PACK = 4
+K_PASS = P * PACK
+BANK = 512
+
+C = 1024
+PASSES = C // K_PASS
+CK = 256
+CV = 256
+HALVES = CK // P
+H = 24
+W = 48
+N = H * W
+EPS = 1e-5
+
+CHUNK_ROWS = 8
+CHUNK = CHUNK_ROWS * W
+CHUNKS = N // CHUNK
+TILES = CHUNK // P
+ALL_TILES = CHUNKS * TILES
+
+LEVELS = (1, 3, 6, 8)
+FIRST = {1: 0, 3: 1, 6: 10, 8: 46}
+TOKENS = 110
+
+FLOPS = 2 * (CK + CV) * C * N
+
+
+LAG_QUANTISE = 1
+LAG_PROJECT = 3
+LAG_LEAVE = 5
+LAG_POOL_VALUES = 7
+LAG_POOL_KEYS = 8
+LAST_TURN = ALL_TILES + LAG_POOL_KEYS
+POOLED = (8, 6, 3)
+
+
+def tile_apnb_pa_kernel(tc, feats, Wk, bk, gk, betak, mk, vk, Wv, bv, out_0, out_1, out_2):
+    nc = tc.nc
+    with ExitStack() as ctx:
+        keep = ctx.enter_context(tc.tile_pool(name="keep", bufs=1))
+        key_banks = ctx.enter_context(tc.psum_pool(name="key_banks", bufs=2 * HALVES))
+        val_banks = ctx.enter_context(tc.psum_pool(name="val_banks", bufs=3))
+        total = ctx.enter_context(tc.psum_pool(name="total", bufs=1))
+        ctx.enter_context(tc.manual_schedule())
+
+        bv_row_bf = keep.tile([P, CV], BF16, name="bv_row_bf")
+        nc.gpsimd.memset(bv_row_bf[:], 0.0)
+        position = keep.tile([P, ALL_TILES], I32, name="position")
+        nc.gpsimd.iota(position[:], pattern=[[P, ALL_TILES]], base=0, channel_multiplier=1)
+        count = keep.tile([P, 64], F32, name="count")
+        nc.gpsimd.iota(
+            count[:], pattern=[[1, 64]], base=0, channel_multiplier=0, allow_small_or_imprecise_dtypes=True
+        )
+        ident = keep.tile([P, P], F32, name="ident")
+        make_identity(nc, ident[:])
+        cell_size = keep.tile([P, P], F32, name="cell_size")
+        nc.gpsimd.memset(cell_size[:, TOKENS:P], 1.0)
+        for s in LEVELS:
+            nc.gpsimd.memset(cell_size[:, FIRST[s] : FIRST[s] + s * s], float(N // (s * s)))
+        bias_pick = keep.tile([P, P], F32, name="bias_pick")
+        nc.gpsimd.tensor_scalar(
+            out=bias_pick[:], in0=cell_size[:], scalar1=ident[:, 0:1], scalar2=0.0, op0=ALU.mult, op1=ALU.add
+        )
+
+        by_channel = keep.tile([P, 5, 16], BF16, name="by_channel")
+        for v, values in enumerate((bk, gk, betak, mk, vk)):
+            nc.scalar.dma_start(out=by_channel[:, v, 0:HALVES], in_=values.rearrange("(p m) -> p m", m=HALVES))
+        nc.scalar.dma_start(out=bv_row_bf[0:1, :], in_=bv.rearrange("(o c) -> o c", o=1))
+
+        def load_weight(rows_by_partition, name):
+            rows = keep.tile([P, HALVES, C], BF16, name=name)
+            nc.sync.dma_start(out=rows[:], in_=rows_by_partition)
+            return rows
+
+        wk_rows = load_weight(Wk.rearrange("(p r) k -> p r k", r=HALVES), "wk_rows")
+
+        x_rows = feats.rearrange("b (g q t) h w -> q (b g) t (h w)", g=PASSES, t=PACK)
+        raw = [keep.tile([P, PASSES, PACK, CHUNK], BF16, name="raw%d" % c) for c in range(CHUNKS)]
+
+        def load_chunk(c):
+            for g in range(PASSES):
+                nc.sync.dma_start(out=raw[c][:, g], in_=x_rows[:, g, :, c * CHUNK : (c + 1) * CHUNK])
+
+        load_chunk(0)
+        wv_rows = load_weight(Wv.rearrange("(r p) k -> p r k", p=P), "wv_rows")
+        load_chunk(1)
+        load_chunk(2)
+
+        shifted = keep.tile([P, 2, ALL_TILES], I32, name="shifted")
+        product = keep.tile([P, 2, ALL_TILES], I32, name="product")
+
+        def third(out, in_, also_shift_left):
+            like = product[:, 0 : in_.shape[1], :]
+            nc.vector.tensor_scalar(out=like, in0=in_, scalar1=683.0, scalar2=None, op0=ALU.mult)
+            nc.vector.tensor_scalar(
+                out=out,
+                in0=like,
+                scalar1=11,
+                scalar2=also_shift_left,
+                op0=ALU.logical_shift_right,
+                op1=ALU.logical_shift_left,
+            )
+
+        place = keep.tile([P, 2, ALL_TILES], I32, name="place")
+        nc.vector.tensor_scalar(
+            out=shifted[:, 0:1, :], in0=position[:].unsqueeze(1), scalar1=4, scalar2=None, op0=ALU.logical_shift_right
+        )
+        third(place[:, 0:1, :], shifted[:, 0:1, :], 1)
+        nc.vector.scalar_tensor_tensor(
+            out=place[:, 1, :], in0=place[:, 0, :], scalar=-24.0, in1=position[:], op0=ALU.mult, op1=ALU.add
+        )
+        band_cell = keep.tile([P, 3, 2, ALL_TILES], I32, name="band_cell")
+        nc.vector.tensor_scalar(out=band_cell[:, 0], in0=place[:], scalar1=4, scalar2=None, op0=ALU.logical_shift_right)
+        nc.vector.tensor_scalar(out=band_cell[:, 1], in0=place[:], scalar1=3, scalar2=None, op0=ALU.logical_shift_right)
+        nc.vector.tensor_scalar(out=shifted[:], in0=place[:], scalar1=1, scalar2=None, op0=ALU.logical_shift_right)
+        third(band_cell[:, 2], shifted[:], 0)
+        cell = keep.tile([P, 3, ALL_TILES], F32, name="cell")
+        pool = keep.tile([P, ALL_TILES, P], F32, name="pool")
+        nc.vector.memset(pool[:, :, 0:1], 1.0)
+        nc.vector.memset(pool[:, :, TOKENS:P], 0.0)
+        for l, s in enumerate(LEVELS[1:]):
+            nc.vector.scalar_tensor_tensor(
+                out=cell[:, l, :],
+                in0=band_cell[:, l, 0, :],
+                scalar=float(s),
+                in1=band_cell[:, l, 1, :],
+                op0=ALU.mult,
+                op1=ALU.add,
+            )
+            shape = [P, ALL_TILES, s * s]
+            nc.vector.tensor_tensor(
+                out=pool[:, :, FIRST[s] : FIRST[s] + s * s],
+                in0=count[:, 0 : s * s].unsqueeze(1).to_broadcast(shape),
+                in1=cell[:, l, :].unsqueeze(2).to_broadcast(shape),
+                op=ALU.is_equal,
+            )
+        weight = keep.tile([P, P], F32, name="weight")
+        nc.vector.reciprocal(out=weight[:], in_=cell_size[:])
+
+        def flip_weight(rows, name, psum, tag, copies):
+            w_grouped = keep.tile([P, PASSES, HALVES * P, PACK], BF16, name=name + "_grouped", align_bytes=64)
+            w_pairs = w_grouped[:].bitcast(F32)
+            for r, copy in enumerate(copies):
+                words = rows[:, r, :].bitcast(F32)
+                bank = psum.tile([P, BANK], F32, name=name + "_bank", tag=tag)
+                for g in range(PASSES):
+                    for u in range(2):
+                        s = 2 * g + u
+                        every_second = words[:, 2 * P * g + u : 2 * P * (g + 1) : 2]
+                        nc.tensor.transpose(bank[:, s * P : (s + 1) * P], every_second, ident[:])
+                copy(
+                    out=w_pairs[:, :, r * P : (r + 1) * P, :],
+                    in_=bank[:].rearrange("p (g u o) -> p g o u", g=PASSES, u=2),
+                )
+            return w_grouped
+
+        def quantise_weight(w_grouped, name):
+            codes = keep.tile([P, PASSES, HALVES * P], U32, name=name + "_codes", align_bytes=64)
+            scales = keep.tile([P, PASSES, HALVES * P], U8, name=name + "_scales", align_bytes=64)
+            nc.vector.quantize_mx(
+                out=codes[:].rearrange("p g o -> p (g o)").bitcast(FP8X4),
+                scales=scales[:].rearrange("p g o -> p (g o)"),
+                in_=w_grouped[:].rearrange("p g o t -> p (g o t)"),
+            )
+            return codes, scales
+
+        wk_grouped = flip_weight(wk_rows, "wk", key_banks, "keys", (nc.vector.tensor_copy, nc.scalar.copy))
+
+        bk_c, gk_c, betak_c, mk_c, vk_c = [by_channel[:, v, 0:HALVES] for v in range(5)]
+        minus_half = keep.tile([P, HALVES], F32, name="minus_half")
+        nc.gpsimd.memset(minus_half[:], -0.5)
+        scale = keep.tile([P, HALVES], F32, name="scale")
+        shift = keep.tile([P, HALVES], F32, name="shift")
+        nc.gpsimd.tensor_scalar_add(out=scale[:], in0=vk_c, scalar1=EPS)
+        nc.gpsimd.tensor_tensor(out=scale[:], in0=scale[:], in1=minus_half[:], op=ALU.pow)
+        nc.gpsimd.tensor_mul(out=scale[:], in0=scale[:], in1=gk_c)
+        nc.gpsimd.tensor_sub(out=shift[:], in0=bk_c, in1=mk_c)
+        nc.gpsimd.tensor_mul(out=shift[:], in0=shift[:], in1=scale[:])
+        nc.gpsimd.tensor_add(out=shift[:], in0=shift[:], in1=betak_c)
+
+        weight_bank = val_banks.tile([P, BANK], F32, name="weight_bank", tag="vals")
+        nc.tensor.transpose(weight_bank[:, 0:P], weight[:], ident[:])
+        token_weight = keep.tile([P, 1], F32, name="token_weight")
+        bv_row = keep.tile([P, CV], F32, name="bv_row")
+        nc.gpsimd.tensor_scalar(out=bv_row[:], in0=bv_row_bf[:], scalar1=1.0, scalar2=0.0, op0=ALU.mult, op1=ALU.add)
+        value_sum = total.tile([P, BANK], F32, name="value_sum")
+
+        grouped = keep.tile([P, ALL_TILES, PASSES, P, PACK], BF16, name="grouped", align_bytes=64)
+        x_codes = keep.tile([P, ALL_TILES, PASSES, P], U32, name="x_codes", align_bytes=64)
+        x_scales = keep.tile([P, ALL_TILES, PASSES, P], U8, name="x_scales", align_bytes=64)
+        kf = keep.tile([P, HALVES, N], F32, name="kf")
+        kf_out = out_0.rearrange("b (p m) h w -> p (b m) (h w)", m=HALVES)
+        pairs = keep.tile([P, HALVES, N // 2], F32, name="pairs")
+        sums = keep.tile([P, HALVES, TOKENS], F32, name="sums")
+        val_t = keep.tile([P, ALL_TILES, CV], F32, name="val_t")
+        key_bank = {}
+        val_bank = {}
+
+        def regroup(i):
+            c, j = divmod(i, TILES)
+            for g, copy in enumerate((nc.vector.tensor_copy, nc.scalar.copy)):
+                copy(
+                    out=grouped[:, i, g].rearrange("p (n r) t -> p n t r", r=4),
+                    in_=raw[c][:, g, :, j * P : (j + 1) * P].rearrange("p t (n r) -> p n t r", r=4),
+                )
+
+        def quantise(i):
+            nc.vector.quantize_mx(
+                out=x_codes[:, i].rearrange("p g n -> p (g n)").bitcast(FP8X4),
+                scales=x_scales[:, i].rearrange("p g n -> p (g n)"),
+                in_=grouped[:, i].rearrange("p g n t -> p (g n t)"),
+            )
+
+        def project_keys(i):
+            c, j = divmod(i, TILES)
+            for m in range(HALVES):
+                if j == 0:
+                    key_bank[c, m] = key_banks.tile([P, BANK], F32, name="key_bank", tag="keys")
+                for g in range(PASSES):
+                    nc.tensor.matmul_mx(
+                        out=key_bank[c, m][:, j * P : (j + 1) * P],
+                        lhsT=wk_codes[:, g, m * P : (m + 1) * P].bitcast(FP8X4),
+                        lhsT_scale=wk_scales[:, g, m * P : (m + 1) * P],
+                        rhs=x_codes[:, i, g, :].bitcast(FP8X4),
+                        rhs_scale=x_scales[:, i, g, :],
+                        start=(g == 0),
+                        stop=(g == PASSES - 1),
+                    )
+
+        def project_values(i):
+            val_bank[i] = val_banks.tile([P, BANK], F32, name="val_bank", tag="vals")
+            for g in range(PASSES):
+                nc.tensor.matmul_mx(
+                    out=val_bank[i][:, 0:CV],
+                    lhsT=x_codes[:, i, g, :].bitcast(FP8X4),
+                    lhsT_scale=x_scales[:, i, g, :],
+                    rhs=wv_codes[:, g, :].bitcast(FP8X4),
+                    rhs_scale=wv_scales[:, g, :],
+                    start=(g == 0),
+                    stop=(g == PASSES - 1),
+                )
+
+        def leave_values(i):
+            nc.scalar.copy(out=val_t[:, i, :], in_=val_bank[i][:, 0:CV])
+
+        def leave_keys(i):
+            c, j = divmod(i, TILES)
+            if j == TILES - 1:
+                cols = slice(c * CHUNK, (c + 1) * CHUNK)
+                for m in range(HALVES):
+                    nc.scalar.activation(
+                        out=kf[:, m, cols],
+                        in_=key_bank[c, m][:, 0:CHUNK],
+                        func=ACT.Relu,
+                        bias=shift[:, m : m + 1],
+                        scale=scale[:, m : m + 1],
+                    )
+                nc.sync.dma_start(out=kf_out[:, :, cols], in_=kf[:, :, cols])
+
+        def pool_values(i):
+            if i == 0:
+                nc.tensor.matmul(out=value_sum[:, 0:CV], lhsT=bias_pick[:], rhs=bv_row[:], start=True, stop=False)
+            nc.tensor.matmul(
+                out=value_sum[:, 0:CV], lhsT=pool[:, i, :], rhs=val_t[:, i, :], start=False, stop=(i == ALL_TILES - 1)
+            )
+
+        def pool_keys(i):
+            c, j = divmod(i, TILES)
+            s = POOLED[j]
+            if s == 3:
+                nc.vector.tensor_reduce(
+                    out=sums[:, :, FIRST[3] + 3 * c : FIRST[3] + 3 * (c + 1)],
+                    in_=sums[:, :, FIRST[6] + 12 * c : FIRST[6] + 12 * (c + 1)].rearrange(
+                        "p m (b c x) -> p m c b x", b=2, x=2
+                    ),
+                    axis=AXIS.XY,
+                    op=ALU.add,
+                )
+                return
+            if s == POOLED[0]:
+                two = kf[:, :, c * CHUNK : (c + 1) * CHUNK].rearrange("p m (q e) -> p m q e", e=2)
+                nc.vector.tensor_tensor(
+                    out=pairs[:, :, c * CHUNK // 2 : (c + 1) * CHUNK // 2], in0=two[:, :, :, 0], in1=two[:, :, :, 1], op=ALU.add
+                )
+            rows = H // s
+            first = c * CHUNK_ROWS // rows
+            after = (c + 1) * CHUNK_ROWS // rows
+            for m in range(HALVES):
+                nc.vector.tensor_reduce(
+                    out=sums[:, m, FIRST[s] + first * s : FIRST[s] + after * s].rearrange("p (b c) -> p b c", c=s),
+                    in_=pairs[:, m, first * rows * W // 2 : after * rows * W // 2].rearrange(
+                        "p (b r c x) -> p b c r x", r=rows, c=s, x=W // s // 2
+                    ),
+                    axis=AXIS.XY,
+                    op=ALU.add,
+                )
+
+        def due(turn, lag):
+            return 0 <= turn - lag < ALL_TILES
+
+        def take_turn(turn):
+            if due(turn, LAG_PROJECT):
+                project_keys(turn - LAG_PROJECT)
+                project_values(turn - LAG_PROJECT)
+            if due(turn, LAG_LEAVE):
+                leave_keys(turn - LAG_LEAVE)
+                leave_values(turn - LAG_LEAVE)
+            if due(turn, LAG_POOL_VALUES):
+                pool_values(turn - LAG_POOL_VALUES)
+            if due(turn, LAG_POOL_KEYS):
+                pool_keys(turn - LAG_POOL_KEYS)
+            if due(turn, LAG_QUANTISE):
+                quantise(turn - LAG_QUANTISE)
+            if due(turn, 0):
+                regroup(turn)
+
+        take_turn(0)
+        nc.scalar.copy(out=token_weight[:], in_=weight_bank[:, 0:1])
+        wk_codes, wk_scales = quantise_weight(wk_grouped, "wk")
+        take_turn(1)
+        take_turn(2)
+        wv_codes, wv_scales = quantise_weight(flip_weight(wv_rows, "wv", val_banks, "vals", (nc.scalar.copy, nc.scalar.copy)), "wv")
+        for turn in range(3, LAST_TURN):
+            take_turn(turn)
+
+        value = keep.tile([P, CV], F32, name="value")
+        nc.scalar.activation(out=value[:], in_=value_sum[:, 0:CV], func=ACT.Copy, scale=token_weight[:, 0:1])
+        nc.sync.dma_start(out=out_2.rearrange("b t c -> (b t) c"), in_=value[0:TOKENS, :])
+
+        nc.vector.tensor_reduce(out=sums[:, :, 0:1], in_=sums[:, :, FIRST[3] : FIRST[6]], axis=AXIS.X, op=ALU.add)
+        keyp = keep.tile([P, HALVES, TOKENS], F32, name="keyp")
+        nc.vector.tensor_tensor(
+            out=keyp[:],
+            in0=sums[:],
+            in1=weight[:, 0:TOKENS].unsqueeze(1).to_broadcast([P, HALVES, TOKENS]),
+            op=ALU.mult,
+        )
+        nc.sync.dma_start(out=out_1.rearrange("b (p m) t -> p (b m) t", m=HALVES), in_=keyp[:])

@@ -28,11 +28,10 @@ W = 48
 N = H * W
 EPS = 1e-5
 
-CHUNK_ROWS = 8
-CHUNK = CHUNK_ROWS * W
-CHUNKS = N // CHUNK
-TILES = CHUNK // P
-ALL_TILES = CHUNKS * TILES
+UNITS = ((0, 256), (256, 256), (512, 256), (768, 256), (1024, 128))
+N_UNITS = len(UNITS)
+LOADS = ((0, 512), (512, 640))
+LOAD_OF = (0, 0, 1, 1, 1)
 
 LEVELS = (1, 3, 6, 8)
 FIRST = {1: 0, 3: 1, 6: 10, 8: 46}
@@ -41,69 +40,81 @@ TOKENS = 110
 FLOPS = 2 * (CK + CV) * C * N
 
 
-LAG_QUANTISE = 1
-LAG_PROJECT = 3
-LAG_LEAVE = 5
-LAG_POOL_VALUES = 7
-LAG_POOL_KEYS = 8
-LAST_TURN = ALL_TILES + LAG_POOL_KEYS
-POOLED = (8, 6, 3)
-
-
 def tile_apnb_pa_kernel(tc, feats, Wk, bk, gk, betak, mk, vk, Wv, bv, out_0, out_1, out_2):
     nc = tc.nc
     with ExitStack() as ctx:
         keep = ctx.enter_context(tc.tile_pool(name="keep", bufs=1))
-        key_banks = ctx.enter_context(tc.psum_pool(name="key_banks", bufs=2 * HALVES))
+        key_banks = ctx.enter_context(tc.psum_pool(name="key_banks", bufs=4))
         val_banks = ctx.enter_context(tc.psum_pool(name="val_banks", bufs=3))
         total = ctx.enter_context(tc.psum_pool(name="total", bufs=1))
         ctx.enter_context(tc.manual_schedule())
 
-        bv_row_bf = keep.tile([P, CV], BF16, name="bv_row_bf")
-        nc.gpsimd.memset(bv_row_bf[:], 0.0)
-        position = keep.tile([P, ALL_TILES], I32, name="position")
-        nc.gpsimd.iota(position[:], pattern=[[P, ALL_TILES]], base=0, channel_multiplier=1)
-        count = keep.tile([P, 64], F32, name="count")
-        nc.gpsimd.iota(
-            count[:], pattern=[[1, 64]], base=0, channel_multiplier=0, allow_small_or_imprecise_dtypes=True
-        )
-        ident = keep.tile([P, P], F32, name="ident")
-        make_identity(nc, ident[:])
-        cell_size = keep.tile([P, P], F32, name="cell_size")
-        nc.gpsimd.memset(cell_size[:, TOKENS:P], 1.0)
-        for s in LEVELS:
-            nc.gpsimd.memset(cell_size[:, FIRST[s] : FIRST[s] + s * s], float(N // (s * s)))
-        bias_pick = keep.tile([P, P], F32, name="bias_pick")
-        nc.gpsimd.tensor_scalar(
-            out=bias_pick[:], in0=cell_size[:], scalar1=ident[:, 0:1], scalar2=0.0, op0=ALU.mult, op1=ALU.add
-        )
-
+        bv_row = keep.tile([P, CV], BF16, name="bv_row")
+        nc.gpsimd.memset(bv_row[:], 0.0)
         by_channel = keep.tile([P, 5, 16], BF16, name="by_channel")
-        for v, values in enumerate((bk, gk, betak, mk, vk)):
-            nc.scalar.dma_start(out=by_channel[:, v, 0:HALVES], in_=values.rearrange("(p m) -> p m", m=HALVES))
-        nc.scalar.dma_start(out=bv_row_bf[0:1, :], in_=bv.rearrange("(o c) -> o c", o=1))
+
+        x_rows = feats.rearrange("b (g q t) h w -> q (b g) t (h w)", g=PASSES, t=PACK)
+        raw = [keep.tile([P, PASSES, PACK, n], BF16, name="raw%d" % i) for i, (first, n) in enumerate(LOADS)]
+
+        def load_feats(i, g):
+            first, n = LOADS[i]
+            nc.sync.dma_start(out=raw[i][:, g], in_=x_rows[:, g, :, first : first + n])
 
         def load_weight(rows_by_partition, name):
             rows = keep.tile([P, HALVES, C], BF16, name=name)
             nc.sync.dma_start(out=rows[:], in_=rows_by_partition)
             return rows
 
+        for g in range(PASSES):
+            load_feats(0, g)
         wk_rows = load_weight(Wk.rearrange("(p r) k -> p r k", r=HALVES), "wk_rows")
-
-        x_rows = feats.rearrange("b (g q t) h w -> q (b g) t (h w)", g=PASSES, t=PACK)
-        raw = [keep.tile([P, PASSES, PACK, CHUNK], BF16, name="raw%d" % c) for c in range(CHUNKS)]
-
-        def load_chunk(c):
-            for g in range(PASSES):
-                nc.sync.dma_start(out=raw[c][:, g], in_=x_rows[:, g, :, c * CHUNK : (c + 1) * CHUNK])
-
-        load_chunk(0)
+        for v, values in enumerate((bk, gk, betak, mk, vk)):
+            nc.sync.dma_start(out=by_channel[:, v, 0:HALVES], in_=values.rearrange("(p m) -> p m", m=HALVES))
         wv_rows = load_weight(Wv.rearrange("(r p) k -> p r k", p=P), "wv_rows")
-        load_chunk(1)
-        load_chunk(2)
+        for g in range(PASSES):
+            load_feats(1, g)
+        nc.sync.dma_start(out=bv_row[0:1, :], in_=bv.rearrange("(o c) -> o c", o=1))
 
-        shifted = keep.tile([P, 2, ALL_TILES], I32, name="shifted")
-        product = keep.tile([P, 2, ALL_TILES], I32, name="product")
+        warm = keep.tile([P, 1], F32, name="warm")
+        nc.vector.memset(warm[:], 0.0)
+        nc.scalar.activation(out=warm[:], in_=warm[:], func=ACT.Relu)
+        place_of = keep.tile([P, N_UNITS], I32, name="place_of")
+        nc.gpsimd.iota(place_of[:, 0 : N_UNITS - 1], pattern=[[2 * P, N_UNITS - 1]], base=0, channel_multiplier=2)
+        nc.gpsimd.iota(place_of[:, N_UNITS - 1 : N_UNITS], pattern=[[0, 1]], base=UNITS[-1][0], channel_multiplier=1)
+        count = keep.tile([P, 64], F32, name="count")
+        nc.gpsimd.iota(
+            count[:], pattern=[[1, 64]], base=0, channel_multiplier=0, allow_small_or_imprecise_dtypes=True
+        )
+        ident = keep.tile([P, P], F32, name="ident")
+        make_identity(nc, ident[:])
+        bias_pick = keep.tile([P, P], BF16, name="bias_pick")
+        nc.gpsimd.memset(bias_pick[:], 0.0)
+        weight = keep.tile([P, TOKENS], F32, name="weight")
+        for s in LEVELS:
+            nc.gpsimd.memset(bias_pick[0:1, FIRST[s] : FIRST[s] + s * s], float(N // (s * s)))
+            nc.gpsimd.tensor_scalar(
+                out=weight[:, FIRST[s] : FIRST[s] + s * s], in0=count[:, 0 : s * s], scalar1=0.0, scalar2=float(s * s) / N,
+                op0=ALU.mult, op1=ALU.add,
+            )
+        token = keep.tile([P, 1], F32, name="token")
+        nc.gpsimd.iota(
+            token[:], pattern=[[0, 1]], base=0, channel_multiplier=1, allow_small_or_imprecise_dtypes=True
+        )
+        token_weight = keep.tile([P, 1], F32, name="token_weight")
+        nc.gpsimd.memset(token_weight[:], 1.0)
+        rise = keep.tile([P, 1], F32, name="rise")
+        for below, s in zip(LEVELS, LEVELS[1:]):
+            nc.gpsimd.tensor_scalar(
+                out=rise[:], in0=token[:], scalar1=float(FIRST[s]), scalar2=float(s * s - below * below),
+                op0=ALU.is_ge, op1=ALU.mult,
+            )
+            nc.gpsimd.tensor_add(out=token_weight[:], in0=token_weight[:], in1=rise[:])
+        nc.gpsimd.tensor_scalar(
+            out=token_weight[:], in0=token_weight[:], scalar1=1.0 / N, scalar2=0.0, op0=ALU.mult, op1=ALU.add
+        )
+
+        shifted = keep.tile([P, 2, N_UNITS], I32, name="shifted")
+        product = keep.tile([P, 2, N_UNITS], I32, name="product")
 
         def third(out, in_, also_shift_left):
             like = product[:, 0 : in_.shape[1], :]
@@ -117,21 +128,21 @@ def tile_apnb_pa_kernel(tc, feats, Wk, bk, gk, betak, mk, vk, Wv, bv, out_0, out
                 op1=ALU.logical_shift_left,
             )
 
-        place = keep.tile([P, 2, ALL_TILES], I32, name="place")
+        place = keep.tile([P, 2, N_UNITS], I32, name="place")
         nc.vector.tensor_scalar(
-            out=shifted[:, 0:1, :], in0=position[:].unsqueeze(1), scalar1=4, scalar2=None, op0=ALU.logical_shift_right
+            out=shifted[:, 0:1, :], in0=place_of[:].unsqueeze(1), scalar1=4, scalar2=None, op0=ALU.logical_shift_right
         )
         third(place[:, 0:1, :], shifted[:, 0:1, :], 1)
         nc.vector.scalar_tensor_tensor(
-            out=place[:, 1, :], in0=place[:, 0, :], scalar=-24.0, in1=position[:], op0=ALU.mult, op1=ALU.add
+            out=place[:, 1, :], in0=place[:, 0, :], scalar=-24.0, in1=place_of[:], op0=ALU.mult, op1=ALU.add
         )
-        band_cell = keep.tile([P, 3, 2, ALL_TILES], I32, name="band_cell")
+        band_cell = keep.tile([P, 3, 2, N_UNITS], I32, name="band_cell")
         nc.vector.tensor_scalar(out=band_cell[:, 0], in0=place[:], scalar1=4, scalar2=None, op0=ALU.logical_shift_right)
         nc.vector.tensor_scalar(out=band_cell[:, 1], in0=place[:], scalar1=3, scalar2=None, op0=ALU.logical_shift_right)
         nc.vector.tensor_scalar(out=shifted[:], in0=place[:], scalar1=1, scalar2=None, op0=ALU.logical_shift_right)
         third(band_cell[:, 2], shifted[:], 0)
-        cell = keep.tile([P, 3, ALL_TILES], F32, name="cell")
-        pool = keep.tile([P, ALL_TILES, P], F32, name="pool")
+        cell = keep.tile([P, 3, N_UNITS], F32, name="cell")
+        pool = keep.tile([P, N_UNITS, P], F32, name="pool")
         nc.vector.memset(pool[:, :, 0:1], 1.0)
         nc.vector.memset(pool[:, :, TOKENS:P], 0.0)
         for l, s in enumerate(LEVELS[1:]):
@@ -143,32 +154,29 @@ def tile_apnb_pa_kernel(tc, feats, Wk, bk, gk, betak, mk, vk, Wv, bv, out_0, out
                 op0=ALU.mult,
                 op1=ALU.add,
             )
-            shape = [P, ALL_TILES, s * s]
+            shape = [P, N_UNITS, s * s]
             nc.vector.tensor_tensor(
                 out=pool[:, :, FIRST[s] : FIRST[s] + s * s],
                 in0=count[:, 0 : s * s].unsqueeze(1).to_broadcast(shape),
                 in1=cell[:, l, :].unsqueeze(2).to_broadcast(shape),
                 op=ALU.is_equal,
             )
-        weight = keep.tile([P, P], F32, name="weight")
-        nc.vector.reciprocal(out=weight[:], in_=cell_size[:])
 
-        def flip_weight(rows, name, psum, tag, copies):
-            w_grouped = keep.tile([P, PASSES, HALVES * P, PACK], BF16, name=name + "_grouped", align_bytes=64)
-            w_pairs = w_grouped[:].bitcast(F32)
-            for r, copy in enumerate(copies):
-                words = rows[:, r, :].bitcast(F32)
-                bank = psum.tile([P, BANK], F32, name=name + "_bank", tag=tag)
-                for g in range(PASSES):
-                    for u in range(2):
-                        s = 2 * g + u
-                        every_second = words[:, 2 * P * g + u : 2 * P * (g + 1) : 2]
-                        nc.tensor.transpose(bank[:, s * P : (s + 1) * P], every_second, ident[:])
-                copy(
-                    out=w_pairs[:, :, r * P : (r + 1) * P, :],
-                    in_=bank[:].rearrange("p (g u o) -> p g o u", g=PASSES, u=2),
-                )
-            return w_grouped
+        def flip_weight(rows, r, psum, tag):
+            words = rows[:, r, :].bitcast(F32)
+            bank = psum.tile([P, BANK], F32, name="flip_bank", tag=tag)
+            for g in range(PASSES):
+                for u in range(2):
+                    s = 2 * g + u
+                    every_second = words[:, 2 * P * g + u : 2 * P * (g + 1) : 2]
+                    nc.tensor.transpose(bank[:, s * P : (s + 1) * P], every_second, ident[:])
+            return bank
+
+        def group_weight(w_grouped, bank, r, copy):
+            copy(
+                out=w_grouped[:].bitcast(F32)[:, :, r * P : (r + 1) * P, :],
+                in_=bank[:].rearrange("p (g u o) -> p g o u", g=PASSES, u=2),
+            )
 
         def quantise_weight(w_grouped, name):
             codes = keep.tile([P, PASSES, HALVES * P], U32, name=name + "_codes", align_bytes=64)
@@ -180,7 +188,8 @@ def tile_apnb_pa_kernel(tc, feats, Wk, bk, gk, betak, mk, vk, Wv, bv, out_0, out
             )
             return codes, scales
 
-        wk_grouped = flip_weight(wk_rows, "wk", key_banks, "keys", (nc.vector.tensor_copy, nc.scalar.copy))
+        wk_grouped = keep.tile([P, PASSES, HALVES * P, PACK], BF16, name="wk_grouped", align_bytes=64)
+        wv_grouped = keep.tile([P, PASSES, HALVES * P, PACK], BF16, name="wv_grouped", align_bytes=64)
 
         bk_c, gk_c, betak_c, mk_c, vk_c = [by_channel[:, v, 0:HALVES] for v in range(5)]
         minus_half = keep.tile([P, HALVES], F32, name="minus_half")
@@ -194,150 +203,181 @@ def tile_apnb_pa_kernel(tc, feats, Wk, bk, gk, betak, mk, vk, Wv, bv, out_0, out
         nc.gpsimd.tensor_mul(out=shift[:], in0=shift[:], in1=scale[:])
         nc.gpsimd.tensor_add(out=shift[:], in0=shift[:], in1=betak_c)
 
-        weight_bank = val_banks.tile([P, BANK], F32, name="weight_bank", tag="vals")
-        nc.tensor.transpose(weight_bank[:, 0:P], weight[:], ident[:])
-        token_weight = keep.tile([P, 1], F32, name="token_weight")
-        bv_row = keep.tile([P, CV], F32, name="bv_row")
-        nc.gpsimd.tensor_scalar(out=bv_row[:], in0=bv_row_bf[:], scalar1=1.0, scalar2=0.0, op0=ALU.mult, op1=ALU.add)
         value_sum = total.tile([P, BANK], F32, name="value_sum")
-
-        grouped = keep.tile([P, ALL_TILES, PASSES, P, PACK], BF16, name="grouped", align_bytes=64)
-        x_codes = keep.tile([P, ALL_TILES, PASSES, P], U32, name="x_codes", align_bytes=64)
-        x_scales = keep.tile([P, ALL_TILES, PASSES, P], U8, name="x_scales", align_bytes=64)
-        kf = keep.tile([P, HALVES, N], F32, name="kf")
+        grouped = []
+        x_codes = []
+        x_scales = []
+        for i, (first, n) in enumerate(UNITS):
+            grouped.append(keep.tile([P, PASSES, n, PACK], BF16, name="grouped%d" % i, align_bytes=64))
+            x_codes.append(keep.tile([P, PASSES, n], U32, name="x_codes%d" % i, align_bytes=64))
+            x_scales.append(keep.tile([P, PASSES, n], U8, name="x_scales%d" % i, align_bytes=64))
+        kf = [keep.tile([P, HALVES, n], F32, name="kf%d" % i) for i, (first, n) in enumerate(UNITS)]
         kf_out = out_0.rearrange("b (p m) h w -> p (b m) (h w)", m=HALVES)
         pairs = keep.tile([P, HALVES, N // 2], F32, name="pairs")
         sums = keep.tile([P, HALVES, TOKENS], F32, name="sums")
-        val_t = keep.tile([P, ALL_TILES, CV], F32, name="val_t")
+        val_t = keep.tile([P, N_UNITS, CV], F32, name="val_t")
         key_bank = {}
         val_bank = {}
 
-        def regroup(i):
-            c, j = divmod(i, TILES)
-            for g, copy in enumerate((nc.vector.tensor_copy, nc.scalar.copy)):
+        def regroup(i, g, copy):
+            first, n = UNITS[i]
+            load = LOAD_OF[i]
+            here = raw[load][:, g, :, first - LOADS[load][0] : first - LOADS[load][0] + n]
+            if n == P:
                 copy(
-                    out=grouped[:, i, g].rearrange("p (n r) t -> p n t r", r=4),
-                    in_=raw[c][:, g, :, j * P : (j + 1) * P].rearrange("p t (n r) -> p n t r", r=4),
+                    out=grouped[i][:, g].rearrange("p (j r) t -> p j t r", r=4),
+                    in_=here.rearrange("p t (j r) -> p j t r", r=4),
+                )
+            else:
+                copy(
+                    out=grouped[i][:, g].rearrange("p (e j r) t -> p e j t r", e=2, r=4),
+                    in_=here.rearrange("p t (j r e) -> p e j t r", e=2, r=4),
                 )
 
         def quantise(i):
             nc.vector.quantize_mx(
-                out=x_codes[:, i].rearrange("p g n -> p (g n)").bitcast(FP8X4),
-                scales=x_scales[:, i].rearrange("p g n -> p (g n)"),
-                in_=grouped[:, i].rearrange("p g n t -> p (g n t)"),
+                out=x_codes[i][:].rearrange("p g n -> p (g n)").bitcast(FP8X4),
+                scales=x_scales[i][:].rearrange("p g n -> p (g n)"),
+                in_=grouped[i][:].rearrange("p g n t -> p (g n t)"),
             )
 
         def project_keys(i):
-            c, j = divmod(i, TILES)
+            first, n = UNITS[i]
+            key_bank[i] = key_banks.tile([P, HALVES, BANK // HALVES], F32, name="key_bank", tag="keys")
             for m in range(HALVES):
-                if j == 0:
-                    key_bank[c, m] = key_banks.tile([P, BANK], F32, name="key_bank", tag="keys")
                 for g in range(PASSES):
                     nc.tensor.matmul_mx(
-                        out=key_bank[c, m][:, j * P : (j + 1) * P],
+                        out=key_bank[i][:, m, 0:n],
                         lhsT=wk_codes[:, g, m * P : (m + 1) * P].bitcast(FP8X4),
                         lhsT_scale=wk_scales[:, g, m * P : (m + 1) * P],
-                        rhs=x_codes[:, i, g, :].bitcast(FP8X4),
-                        rhs_scale=x_scales[:, i, g, :],
+                        rhs=x_codes[i][:, g, :].bitcast(FP8X4),
+                        rhs_scale=x_scales[i][:, g, :],
                         start=(g == 0),
                         stop=(g == PASSES - 1),
                     )
 
         def project_values(i):
+            first, n = UNITS[i]
             val_bank[i] = val_banks.tile([P, BANK], F32, name="val_bank", tag="vals")
-            for g in range(PASSES):
+            steps = [(e, g) for e in range(n // P) for g in range(PASSES)]
+            for e, g in steps:
                 nc.tensor.matmul_mx(
                     out=val_bank[i][:, 0:CV],
-                    lhsT=x_codes[:, i, g, :].bitcast(FP8X4),
-                    lhsT_scale=x_scales[:, i, g, :],
+                    lhsT=x_codes[i][:, g, e * P : (e + 1) * P].bitcast(FP8X4),
+                    lhsT_scale=x_scales[i][:, g, e * P : (e + 1) * P],
                     rhs=wv_codes[:, g, :].bitcast(FP8X4),
                     rhs_scale=wv_scales[:, g, :],
-                    start=(g == 0),
-                    stop=(g == PASSES - 1),
+                    start=((e, g) == steps[0]),
+                    stop=((e, g) == steps[-1]),
                 )
 
         def leave_values(i):
             nc.scalar.copy(out=val_t[:, i, :], in_=val_bank[i][:, 0:CV])
 
         def leave_keys(i):
-            c, j = divmod(i, TILES)
-            if j == TILES - 1:
-                cols = slice(c * CHUNK, (c + 1) * CHUNK)
-                for m in range(HALVES):
-                    nc.scalar.activation(
-                        out=kf[:, m, cols],
-                        in_=key_bank[c, m][:, 0:CHUNK],
-                        func=ACT.Relu,
-                        bias=shift[:, m : m + 1],
-                        scale=scale[:, m : m + 1],
-                    )
-                nc.sync.dma_start(out=kf_out[:, :, cols], in_=kf[:, :, cols])
+            first, n = UNITS[i]
+            for m in range(HALVES):
+                out = kf[i][:, m, :]
+                in_ = key_bank[i][:, m, 0:n]
+                if n > P:
+                    out = out.rearrange("p (j e) -> p j e", e=2)
+                    in_ = in_.rearrange("p (e j) -> p j e", e=2)
+                nc.scalar.activation(
+                    out=out, in_=in_, func=ACT.Relu, bias=shift[:, m : m + 1], scale=scale[:, m : m + 1]
+                )
+            nc.sync.dma_start(out=kf_out[:, :, first : first + n], in_=kf[i][:])
 
         def pool_values(i):
             if i == 0:
                 nc.tensor.matmul(out=value_sum[:, 0:CV], lhsT=bias_pick[:], rhs=bv_row[:], start=True, stop=False)
             nc.tensor.matmul(
-                out=value_sum[:, 0:CV], lhsT=pool[:, i, :], rhs=val_t[:, i, :], start=False, stop=(i == ALL_TILES - 1)
+                out=value_sum[:, 0:CV], lhsT=pool[:, i, :], rhs=val_t[:, i, :], start=False, stop=(i == N_UNITS - 1)
             )
 
         def pool_keys(i):
-            c, j = divmod(i, TILES)
-            s = POOLED[j]
-            if s == 3:
-                nc.vector.tensor_reduce(
-                    out=sums[:, :, FIRST[3] + 3 * c : FIRST[3] + 3 * (c + 1)],
-                    in_=sums[:, :, FIRST[6] + 12 * c : FIRST[6] + 12 * (c + 1)].rearrange(
-                        "p m (b c x) -> p m c b x", b=2, x=2
-                    ),
-                    axis=AXIS.XY,
-                    op=ALU.add,
-                )
-                return
-            if s == POOLED[0]:
-                two = kf[:, :, c * CHUNK : (c + 1) * CHUNK].rearrange("p m (q e) -> p m q e", e=2)
-                nc.vector.tensor_tensor(
-                    out=pairs[:, :, c * CHUNK // 2 : (c + 1) * CHUNK // 2], in0=two[:, :, :, 0], in1=two[:, :, :, 1], op=ALU.add
-                )
-            rows = H // s
-            first = c * CHUNK_ROWS // rows
-            after = (c + 1) * CHUNK_ROWS // rows
-            for m in range(HALVES):
-                nc.vector.tensor_reduce(
-                    out=sums[:, m, FIRST[s] + first * s : FIRST[s] + after * s].rearrange("p (b c) -> p b c", c=s),
-                    in_=pairs[:, m, first * rows * W // 2 : after * rows * W // 2].rearrange(
-                        "p (b r c x) -> p b c r x", r=rows, c=s, x=W // s // 2
-                    ),
-                    axis=AXIS.XY,
-                    op=ALU.add,
-                )
+            first, n = UNITS[i]
+            two = kf[i][:].rearrange("p m (q e) -> p m q e", e=2)
+            nc.vector.tensor_tensor(
+                out=pairs[:, :, first // 2 : (first + n) // 2], in0=two[:, :, :, 0], in1=two[:, :, :, 1], op=ALU.add
+            )
+            for s in (6, 8):
+                band = H // s * W
+                for b in range(first // band, (first + n) // band):
+                    nc.vector.tensor_reduce(
+                        out=sums[:, :, FIRST[s] + b * s : FIRST[s] + (b + 1) * s],
+                        in_=pairs[:, :, b * band // 2 : (b + 1) * band // 2].rearrange(
+                            "p m (r c x) -> p m c r x", r=H // s, c=s
+                        ),
+                        axis=AXIS.XY,
+                        op=ALU.add,
+                    )
+                    if s == 6 and b % 2:
+                        h = b // 2
+                        nc.vector.tensor_reduce(
+                            out=sums[:, :, FIRST[3] + 3 * h : FIRST[3] + 3 * (h + 1)],
+                            in_=sums[:, :, FIRST[6] + 12 * h : FIRST[6] + 12 * (h + 1)].rearrange(
+                                "p m (b c x) -> p m c b x", b=2, x=2
+                            ),
+                            axis=AXIS.XY,
+                            op=ALU.add,
+                        )
 
-        def due(turn, lag):
-            return 0 <= turn - lag < ALL_TILES
+        on_vector = nc.vector.tensor_copy
+        on_scalar = nc.scalar.copy
 
-        def take_turn(turn):
-            if due(turn, LAG_PROJECT):
-                project_keys(turn - LAG_PROJECT)
-                project_values(turn - LAG_PROJECT)
-            if due(turn, LAG_LEAVE):
-                leave_keys(turn - LAG_LEAVE)
-                leave_values(turn - LAG_LEAVE)
-            if due(turn, LAG_POOL_VALUES):
-                pool_values(turn - LAG_POOL_VALUES)
-            if due(turn, LAG_POOL_KEYS):
-                pool_keys(turn - LAG_POOL_KEYS)
-            if due(turn, LAG_QUANTISE):
-                quantise(turn - LAG_QUANTISE)
-            if due(turn, 0):
-                regroup(turn)
-
-        take_turn(0)
-        nc.scalar.copy(out=token_weight[:], in_=weight_bank[:, 0:1])
+        for g in range(PASSES):
+            regroup(0, g, on_vector)
+            regroup(1, g, on_scalar)
+        flipped = flip_weight(wk_rows, 0, key_banks, "keys")
+        group_weight(wk_grouped, flipped, 0, on_vector)
+        flipped = flip_weight(wk_rows, 1, key_banks, "keys")
+        group_weight(wk_grouped, flipped, 1, on_scalar)
+        quantise(0)
+        for r in range(HALVES):
+            flipped = flip_weight(wv_rows, r, val_banks, "vals")
+            group_weight(wv_grouped, flipped, r, on_scalar)
         wk_codes, wk_scales = quantise_weight(wk_grouped, "wk")
-        take_turn(1)
-        take_turn(2)
-        wv_codes, wv_scales = quantise_weight(flip_weight(wv_rows, "wv", val_banks, "vals", (nc.scalar.copy, nc.scalar.copy)), "wv")
-        for turn in range(3, LAST_TURN):
-            take_turn(turn)
+        quantise(1)
+        project_keys(0)
+        regroup(2, 0, on_vector)
+        wv_codes, wv_scales = quantise_weight(wv_grouped, "wv")
+        regroup(2, 1, on_scalar)
+        project_values(0)
+        project_keys(1)
+        project_values(1)
+        regroup(3, 0, on_vector)
+        quantise(2)
+        leave_keys(0)
+        leave_values(0)
+        regroup(3, 1, on_scalar)
+        regroup(4, 0, on_vector)
+        pool_keys(0)
+        quantise(3)
+        project_keys(2)
+        project_values(2)
+        pool_values(0)
+        leave_keys(1)
+        leave_values(1)
+        regroup(4, 1, on_scalar)
+        pool_keys(1)
+        quantise(4)
+        project_keys(3)
+        project_values(3)
+        pool_values(1)
+        leave_keys(2)
+        leave_values(2)
+        project_keys(4)
+        project_values(4)
+        pool_values(2)
+        pool_keys(2)
+        leave_keys(3)
+        leave_values(3)
+        pool_values(3)
+        pool_keys(3)
+        leave_keys(4)
+        leave_values(4)
+        pool_values(4)
+        pool_keys(4)
 
         value = keep.tile([P, CV], F32, name="value")
         nc.scalar.activation(out=value[:], in_=value_sum[:, 0:CV], func=ACT.Copy, scale=token_weight[:, 0:1])
@@ -348,7 +388,7 @@ def tile_apnb_pa_kernel(tc, feats, Wk, bk, gk, betak, mk, vk, Wv, bv, out_0, out
         nc.vector.tensor_tensor(
             out=keyp[:],
             in0=sums[:],
-            in1=weight[:, 0:TOKENS].unsqueeze(1).to_broadcast([P, HALVES, TOKENS]),
+            in1=weight[:].unsqueeze(1).to_broadcast([P, HALVES, TOKENS]),
             op=ALU.mult,
         )
         nc.sync.dma_start(out=out_1.rearrange("b (p m) t -> p (b m) t", m=HALVES), in_=keyp[:])

@@ -30,8 +30,10 @@ EPS = 1e-5
 
 UNITS = ((0, 256), (256, 256), (512, 256), (768, 256), (1024, 128))
 N_UNITS = len(UNITS)
-LOADS = ((0, 512), (512, 640))
-LOAD_OF = (0, 0, 1, 1, 1)
+LOADS = ((0, 512), (512, 512), (1024, 128))
+LOAD_OF = (0, 0, 1, 1, 2)
+
+BANDS_AFTER = ((), (), ((8, 0, 5), (6, 0, 4)), ((8, 5, 7), (6, 4, 5)), ((6, 5, 6), (8, 7, 8)))
 
 LEVELS = (1, 3, 6, 8)
 FIRST = {1: 0, 3: 1, 6: 10, 8: 46}
@@ -49,9 +51,10 @@ def tile_apnb_pa_kernel(tc, feats, Wk, bk, gk, betak, mk, vk, Wv, bv, out_0, out
         total = ctx.enter_context(tc.psum_pool(name="total", bufs=1))
         ctx.enter_context(tc.manual_schedule())
 
-        bv_row = keep.tile([P, CV], BF16, name="bv_row")
-        nc.gpsimd.memset(bv_row[:], 0.0)
-        by_channel = keep.tile([P, 5, 16], BF16, name="by_channel")
+        vectors = keep.tile([P, CV], BF16, name="vectors")
+        nc.gpsimd.memset(vectors[:], 0.0)
+        for row, values in enumerate((bv, bk, gk, betak, mk, vk)):
+            nc.scalar.dma_start(out=vectors[row : row + 1, :], in_=values.rearrange("(o c) -> o c", o=1))
 
         x_rows = feats.rearrange("b (g q t) h w -> q (b g) t (h w)", g=PASSES, t=PACK)
         raw = [keep.tile([P, PASSES, PACK, n], BF16, name="raw%d" % i) for i, (first, n) in enumerate(LOADS)]
@@ -65,15 +68,13 @@ def tile_apnb_pa_kernel(tc, feats, Wk, bk, gk, betak, mk, vk, Wv, bv, out_0, out
             nc.sync.dma_start(out=rows[:], in_=rows_by_partition)
             return rows
 
-        for g in range(PASSES):
-            load_feats(0, g)
+        load_feats(0, 0)
         wk_rows = load_weight(Wk.rearrange("(p r) k -> p r k", r=HALVES), "wk_rows")
-        for v, values in enumerate((bk, gk, betak, mk, vk)):
-            nc.sync.dma_start(out=by_channel[:, v, 0:HALVES], in_=values.rearrange("(p m) -> p m", m=HALVES))
+        load_feats(0, 1)
         wv_rows = load_weight(Wv.rearrange("(r p) k -> p r k", p=P), "wv_rows")
-        for g in range(PASSES):
-            load_feats(1, g)
-        nc.sync.dma_start(out=bv_row[0:1, :], in_=bv.rearrange("(o c) -> o c", o=1))
+        for i in range(1, len(LOADS)):
+            for g in range(PASSES):
+                load_feats(i, g)
 
         warm = keep.tile([P, 1], F32, name="warm")
         nc.vector.memset(warm[:], 0.0)
@@ -113,38 +114,28 @@ def tile_apnb_pa_kernel(tc, feats, Wk, bk, gk, betak, mk, vk, Wv, bv, out_0, out
             out=token_weight[:], in0=token_weight[:], scalar1=1.0 / N, scalar2=0.0, op0=ALU.mult, op1=ALU.add
         )
 
-        shifted = keep.tile([P, 2, N_UNITS], I32, name="shifted")
         product = keep.tile([P, 2, N_UNITS], I32, name="product")
-
-        def third(out, in_, also_shift_left):
-            like = product[:, 0 : in_.shape[1], :]
-            nc.vector.tensor_scalar(out=like, in0=in_, scalar1=683.0, scalar2=None, op0=ALU.mult)
-            nc.vector.tensor_scalar(
-                out=out,
-                in0=like,
-                scalar1=11,
-                scalar2=also_shift_left,
-                op0=ALU.logical_shift_right,
-                op1=ALU.logical_shift_left,
-            )
-
         place = keep.tile([P, 2, N_UNITS], I32, name="place")
+        nc.vector.tensor_scalar(out=product[:, 0, :], in0=place_of[:], scalar1=1366.0, scalar2=None, op0=ALU.mult)
         nc.vector.tensor_scalar(
-            out=shifted[:, 0:1, :], in0=place_of[:].unsqueeze(1), scalar1=4, scalar2=None, op0=ALU.logical_shift_right
+            out=place[:, 0, :],
+            in0=product[:, 0, :],
+            scalar1=16,
+            scalar2=1,
+            op0=ALU.logical_shift_right,
+            op1=ALU.logical_shift_left,
         )
-        third(place[:, 0:1, :], shifted[:, 0:1, :], 1)
         nc.vector.scalar_tensor_tensor(
             out=place[:, 1, :], in0=place[:, 0, :], scalar=-24.0, in1=place_of[:], op0=ALU.mult, op1=ALU.add
         )
         band_cell = keep.tile([P, 3, 2, N_UNITS], I32, name="band_cell")
+        nc.vector.tensor_scalar(out=product[:], in0=place[:], scalar1=683.0, scalar2=None, op0=ALU.mult)
         nc.vector.tensor_scalar(out=band_cell[:, 0], in0=place[:], scalar1=4, scalar2=None, op0=ALU.logical_shift_right)
         nc.vector.tensor_scalar(out=band_cell[:, 1], in0=place[:], scalar1=3, scalar2=None, op0=ALU.logical_shift_right)
-        nc.vector.tensor_scalar(out=shifted[:], in0=place[:], scalar1=1, scalar2=None, op0=ALU.logical_shift_right)
-        third(band_cell[:, 2], shifted[:], 0)
+        nc.vector.tensor_scalar(out=band_cell[:, 2], in0=product[:], scalar1=12, scalar2=None, op0=ALU.logical_shift_right)
         cell = keep.tile([P, 3, N_UNITS], F32, name="cell")
         pool = keep.tile([P, N_UNITS, P], F32, name="pool")
-        nc.vector.memset(pool[:, :, 0:1], 1.0)
-        nc.vector.memset(pool[:, :, TOKENS:P], 0.0)
+        nc.gpsimd.memset(pool[:], 1.0)
         for l, s in enumerate(LEVELS[1:]):
             nc.vector.scalar_tensor_tensor(
                 out=cell[:, l, :],
@@ -191,7 +182,12 @@ def tile_apnb_pa_kernel(tc, feats, Wk, bk, gk, betak, mk, vk, Wv, bv, out_0, out
         wk_grouped = keep.tile([P, PASSES, HALVES * P, PACK], BF16, name="wk_grouped", align_bytes=64)
         wv_grouped = keep.tile([P, PASSES, HALVES * P, PACK], BF16, name="wv_grouped", align_bytes=64)
 
-        bk_c, gk_c, betak_c, mk_c, vk_c = [by_channel[:, v, 0:HALVES] for v in range(5)]
+        by_channel = keep.tile([P, 6], F32, name="by_channel")
+        vector_bank = val_banks.tile([P, BANK], F32, name="vector_bank", tag="vals")
+        nc.tensor.transpose(vector_bank[:, 0:P], vectors[:].bitcast(F32), ident[:])
+        nc.scalar.copy(out=by_channel[:], in_=vector_bank[:, 0:6])
+        pair_of = by_channel[:].bitcast(BF16)
+        bk_c, gk_c, betak_c, mk_c, vk_c = [pair_of[:, HALVES * v : HALVES * (v + 1)] for v in range(1, 6)]
         minus_half = keep.tile([P, HALVES], F32, name="minus_half")
         nc.gpsimd.memset(minus_half[:], -0.5)
         scale = keep.tile([P, HALVES], F32, name="scale")
@@ -289,7 +285,7 @@ def tile_apnb_pa_kernel(tc, feats, Wk, bk, gk, betak, mk, vk, Wv, bv, out_0, out
 
         def pool_values(i):
             if i == 0:
-                nc.tensor.matmul(out=value_sum[:, 0:CV], lhsT=bias_pick[:], rhs=bv_row[:], start=True, stop=False)
+                nc.tensor.matmul(out=value_sum[:, 0:CV], lhsT=bias_pick[:], rhs=vectors[:], start=True, stop=False)
             nc.tensor.matmul(
                 out=value_sum[:, 0:CV], lhsT=pool[:, i, :], rhs=val_t[:, i, :], start=False, stop=(i == N_UNITS - 1)
             )
@@ -300,84 +296,93 @@ def tile_apnb_pa_kernel(tc, feats, Wk, bk, gk, betak, mk, vk, Wv, bv, out_0, out
             nc.vector.tensor_tensor(
                 out=pairs[:, :, first // 2 : (first + n) // 2], in0=two[:, :, :, 0], in1=two[:, :, :, 1], op=ALU.add
             )
-            for s in (6, 8):
-                band = H // s * W
-                for b in range(first // band, (first + n) // band):
+            for s, b0, b1 in BANDS_AFTER[i]:
+                pool_bands(s, b0, b1)
+
+        def pool_bands(s, b0, b1):
+            half_band = H // s * W // 2
+            out = sums[:, :, FIRST[s] + b0 * s : FIRST[s] + b1 * s]
+            in_ = pairs[:, :, b0 * half_band : b1 * half_band]
+            if b1 - b0 == 1:
+                nc.vector.tensor_reduce(
+                    out=out, in_=in_.rearrange("p m (r c x) -> p m c r x", r=H // s, c=s), axis=AXIS.XY, op=ALU.add
+                )
+            else:
+                for m in range(HALVES):
                     nc.vector.tensor_reduce(
-                        out=sums[:, :, FIRST[s] + b * s : FIRST[s] + (b + 1) * s],
-                        in_=pairs[:, :, b * band // 2 : (b + 1) * band // 2].rearrange(
-                            "p m (r c x) -> p m c r x", r=H // s, c=s
-                        ),
+                        out=out[:, m, :].rearrange("p (b c) -> p b c", c=s),
+                        in_=in_[:, m, :].rearrange("p (b r c x) -> p b c r x", b=b1 - b0, r=H // s, c=s),
                         axis=AXIS.XY,
                         op=ALU.add,
                     )
-                    if s == 6 and b % 2:
-                        h = b // 2
-                        nc.vector.tensor_reduce(
-                            out=sums[:, :, FIRST[3] + 3 * h : FIRST[3] + 3 * (h + 1)],
-                            in_=sums[:, :, FIRST[6] + 12 * h : FIRST[6] + 12 * (h + 1)].rearrange(
-                                "p m (b c x) -> p m c b x", b=2, x=2
-                            ),
-                            axis=AXIS.XY,
-                            op=ALU.add,
-                        )
+
+        def pool_thirds(h):
+            nc.vector.tensor_reduce(
+                out=sums[:, :, FIRST[3] + 3 * h : FIRST[3] + 3 * (h + 1)],
+                in_=sums[:, :, FIRST[6] + 12 * h : FIRST[6] + 12 * (h + 1)].rearrange(
+                    "p m (b c x) -> p m c b x", b=2, x=2
+                ),
+                axis=AXIS.XY,
+                op=ALU.add,
+            )
 
         on_vector = nc.vector.tensor_copy
         on_scalar = nc.scalar.copy
 
-        for g in range(PASSES):
-            regroup(0, g, on_vector)
-            regroup(1, g, on_scalar)
-        flipped = flip_weight(wk_rows, 0, key_banks, "keys")
-        group_weight(wk_grouped, flipped, 0, on_vector)
-        flipped = flip_weight(wk_rows, 1, key_banks, "keys")
-        group_weight(wk_grouped, flipped, 1, on_scalar)
+        regroup(0, 0, on_vector)
+        regroup(1, 0, on_scalar)
+        for r, copy in enumerate((on_vector, on_scalar)):
+            group_weight(wk_grouped, flip_weight(wk_rows, r, key_banks, "keys"), r, copy)
+        regroup(0, 1, on_vector)
+        regroup(1, 1, on_scalar)
+        wk_codes, wk_scales = quantise_weight(wk_grouped, "wk")
         quantise(0)
         for r in range(HALVES):
-            flipped = flip_weight(wv_rows, r, val_banks, "vals")
-            group_weight(wv_grouped, flipped, r, on_scalar)
-        wk_codes, wk_scales = quantise_weight(wk_grouped, "wk")
-        quantise(1)
+            group_weight(wv_grouped, flip_weight(wv_rows, r, val_banks, "vals"), r, on_scalar)
         project_keys(0)
         regroup(2, 0, on_vector)
-        wv_codes, wv_scales = quantise_weight(wv_grouped, "wv")
-        regroup(2, 1, on_scalar)
-        project_values(0)
+        quantise(1)
         project_keys(1)
-        project_values(1)
-        regroup(3, 0, on_vector)
-        quantise(2)
         leave_keys(0)
+        wv_codes, wv_scales = quantise_weight(wv_grouped, "wv")
+        project_values(0)
+        project_values(1)
+        regroup(3, 0, on_scalar)
         leave_values(0)
+        regroup(2, 1, on_vector)
+        leave_keys(1)
         regroup(3, 1, on_scalar)
-        regroup(4, 0, on_vector)
         pool_keys(0)
-        quantise(3)
+        quantise(2)
+        leave_values(1)
+        pool_values(0)
         project_keys(2)
         project_values(2)
-        pool_values(0)
-        leave_keys(1)
-        leave_values(1)
-        regroup(4, 1, on_scalar)
+        regroup(4, 0, on_scalar)
         pool_keys(1)
-        quantise(4)
+        regroup(4, 1, on_vector)
+        pool_values(1)
+        quantise(3)
         project_keys(3)
         project_values(3)
-        pool_values(1)
         leave_keys(2)
         leave_values(2)
+        quantise(4)
         project_keys(4)
         project_values(4)
         pool_values(2)
-        pool_keys(2)
         leave_keys(3)
         leave_values(3)
         pool_values(3)
+        pool_keys(2)
+        pool_thirds(0)
+        pool_thirds(1)
         pool_keys(3)
-        leave_keys(4)
         leave_values(4)
+        leave_keys(4)
         pool_values(4)
         pool_keys(4)
+        pool_thirds(2)
 
         value = keep.tile([P, CV], F32, name="value")
         nc.scalar.activation(out=value[:], in_=value_sum[:, 0:CV], func=ACT.Copy, scale=token_weight[:, 0:1])

@@ -33,7 +33,7 @@ N_UNITS = len(UNITS)
 LOADS = ((0, 512), (512, 512), (1024, 128))
 LOAD_OF = (0, 0, 1, 1, 2)
 
-BANDS_AFTER = ((), (), ((8, 0, 5), (6, 0, 4)), ((8, 5, 7), (6, 4, 5)), ((6, 5, 6), (8, 7, 8)))
+BANDS_AFTER = ((), ((8, 0, 3), (6, 0, 2)), ((8, 3, 5), (6, 2, 4)), ((8, 5, 7), (6, 4, 5)), ((6, 5, 6), (8, 7, 8)))
 
 LEVELS = (1, 3, 6, 8)
 FIRST = {1: 0, 3: 1, 6: 10, 8: 46}
@@ -52,9 +52,19 @@ def tile_apnb_pa_kernel(tc, feats, Wk, bk, gk, betak, mk, vk, Wv, bv, out_0, out
         ctx.enter_context(tc.manual_schedule())
 
         vectors = keep.tile([P, CV], BF16, name="vectors")
-        nc.gpsimd.memset(vectors[:], 0.0)
-        for row, values in enumerate((bv, bk, gk, betak, mk, vk)):
-            nc.scalar.dma_start(out=vectors[row : row + 1, :], in_=values.rearrange("(o c) -> o c", o=1))
+        nc.vector.memset(vectors[:], 0.0)
+
+        def load_vectors(queue, first_row, values):
+            for row, value in enumerate(values):
+                queue.dma_start(
+                    out=vectors[first_row + row : first_row + row + 1, :], in_=value.rearrange("(o c) -> o c", o=1)
+                )
+
+        place_of = keep.tile([P, N_UNITS], I32, name="place_of")
+        nc.gpsimd.iota(place_of[:, 0 : N_UNITS - 1], pattern=[[2 * P, N_UNITS - 1]], base=0, channel_multiplier=2)
+        nc.gpsimd.iota(place_of[:, N_UNITS - 1 : N_UNITS], pattern=[[0, 1]], base=UNITS[-1][0], channel_multiplier=1)
+
+        load_vectors(nc.scalar, 0, (bv, bk, gk, betak))
 
         x_rows = feats.rearrange("b (g q t) h w -> q (b g) t (h w)", g=PASSES, t=PACK)
         raw = [keep.tile([P, PASSES, PACK, n], BF16, name="raw%d" % i) for i, (first, n) in enumerate(LOADS)]
@@ -68,20 +78,19 @@ def tile_apnb_pa_kernel(tc, feats, Wk, bk, gk, betak, mk, vk, Wv, bv, out_0, out
             nc.sync.dma_start(out=rows[:], in_=rows_by_partition)
             return rows
 
-        load_feats(0, 0)
         wk_rows = load_weight(Wk.rearrange("(p r) k -> p r k", r=HALVES), "wk_rows")
-        load_feats(0, 1)
+        for g in range(PASSES):
+            load_feats(0, g)
+        load_vectors(nc.sync, 4, (mk, vk))
         wv_rows = load_weight(Wv.rearrange("(r p) k -> p r k", p=P), "wv_rows")
-        for i in range(1, len(LOADS)):
-            for g in range(PASSES):
-                load_feats(i, g)
+        load_feats(1, 0)
+        load_feats(1, 1)
+        for g in range(PASSES):
+            load_feats(2, g)
 
         warm = keep.tile([P, 1], F32, name="warm")
         nc.vector.memset(warm[:], 0.0)
         nc.scalar.activation(out=warm[:], in_=warm[:], func=ACT.Relu)
-        place_of = keep.tile([P, N_UNITS], I32, name="place_of")
-        nc.gpsimd.iota(place_of[:, 0 : N_UNITS - 1], pattern=[[2 * P, N_UNITS - 1]], base=0, channel_multiplier=2)
-        nc.gpsimd.iota(place_of[:, N_UNITS - 1 : N_UNITS], pattern=[[0, 1]], base=UNITS[-1][0], channel_multiplier=1)
         count = keep.tile([P, 64], F32, name="count")
         nc.gpsimd.iota(
             count[:], pattern=[[1, 64]], base=0, channel_multiplier=0, allow_small_or_imprecise_dtypes=True
@@ -90,29 +99,8 @@ def tile_apnb_pa_kernel(tc, feats, Wk, bk, gk, betak, mk, vk, Wv, bv, out_0, out
         make_identity(nc, ident[:])
         bias_pick = keep.tile([P, P], BF16, name="bias_pick")
         nc.gpsimd.memset(bias_pick[:], 0.0)
-        weight = keep.tile([P, TOKENS], F32, name="weight")
         for s in LEVELS:
             nc.gpsimd.memset(bias_pick[0:1, FIRST[s] : FIRST[s] + s * s], float(N // (s * s)))
-            nc.gpsimd.tensor_scalar(
-                out=weight[:, FIRST[s] : FIRST[s] + s * s], in0=count[:, 0 : s * s], scalar1=0.0, scalar2=float(s * s) / N,
-                op0=ALU.mult, op1=ALU.add,
-            )
-        token = keep.tile([P, 1], F32, name="token")
-        nc.gpsimd.iota(
-            token[:], pattern=[[0, 1]], base=0, channel_multiplier=1, allow_small_or_imprecise_dtypes=True
-        )
-        token_weight = keep.tile([P, 1], F32, name="token_weight")
-        nc.gpsimd.memset(token_weight[:], 1.0)
-        rise = keep.tile([P, 1], F32, name="rise")
-        for below, s in zip(LEVELS, LEVELS[1:]):
-            nc.gpsimd.tensor_scalar(
-                out=rise[:], in0=token[:], scalar1=float(FIRST[s]), scalar2=float(s * s - below * below),
-                op0=ALU.is_ge, op1=ALU.mult,
-            )
-            nc.gpsimd.tensor_add(out=token_weight[:], in0=token_weight[:], in1=rise[:])
-        nc.gpsimd.tensor_scalar(
-            out=token_weight[:], in0=token_weight[:], scalar1=1.0 / N, scalar2=0.0, op0=ALU.mult, op1=ALU.add
-        )
 
         product = keep.tile([P, 2, N_UNITS], I32, name="product")
         place = keep.tile([P, 2, N_UNITS], I32, name="place")
@@ -135,7 +123,8 @@ def tile_apnb_pa_kernel(tc, feats, Wk, bk, gk, betak, mk, vk, Wv, bv, out_0, out
         nc.vector.tensor_scalar(out=band_cell[:, 2], in0=product[:], scalar1=12, scalar2=None, op0=ALU.logical_shift_right)
         cell = keep.tile([P, 3, N_UNITS], F32, name="cell")
         pool = keep.tile([P, N_UNITS, P], F32, name="pool")
-        nc.gpsimd.memset(pool[:], 1.0)
+        nc.vector.memset(pool[:, :, 0:1], 1.0)
+        nc.vector.memset(pool[:, :, TOKENS:P], 0.0)
         for l, s in enumerate(LEVELS[1:]):
             nc.vector.scalar_tensor_tensor(
                 out=cell[:, l, :],
@@ -152,6 +141,28 @@ def tile_apnb_pa_kernel(tc, feats, Wk, bk, gk, betak, mk, vk, Wv, bv, out_0, out
                 in1=cell[:, l, :].unsqueeze(2).to_broadcast(shape),
                 op=ALU.is_equal,
             )
+
+        weight = keep.tile([P, TOKENS], F32, name="weight")
+        for s in LEVELS:
+            nc.vector.tensor_scalar(
+                out=weight[:, FIRST[s] : FIRST[s] + s * s],
+                in0=count[:, 0 : s * s],
+                scalar1=0.0,
+                scalar2=float(s * s) / N,
+                op0=ALU.mult,
+                op1=ALU.add,
+            )
+        token_weight = keep.tile([P, 1], F32, name="token_weight")
+        diagonal = keep.tile([P, TOKENS], F32, name="diagonal")
+        nc.vector.scalar_tensor_tensor(
+            out=diagonal[:],
+            in0=ident[:, 0:TOKENS],
+            scalar=1.0,
+            in1=weight[:],
+            op0=ALU.mult,
+            op1=ALU.mult,
+            accum_out=token_weight[:],
+        )
 
         def flip_weight(rows, r, psum, tag):
             words = rows[:, r, :].bitcast(F32)
@@ -181,23 +192,6 @@ def tile_apnb_pa_kernel(tc, feats, Wk, bk, gk, betak, mk, vk, Wv, bv, out_0, out
 
         wk_grouped = keep.tile([P, PASSES, HALVES * P, PACK], BF16, name="wk_grouped", align_bytes=64)
         wv_grouped = keep.tile([P, PASSES, HALVES * P, PACK], BF16, name="wv_grouped", align_bytes=64)
-
-        by_channel = keep.tile([P, 6], F32, name="by_channel")
-        vector_bank = val_banks.tile([P, BANK], F32, name="vector_bank", tag="vals")
-        nc.tensor.transpose(vector_bank[:, 0:P], vectors[:].bitcast(F32), ident[:])
-        nc.scalar.copy(out=by_channel[:], in_=vector_bank[:, 0:6])
-        pair_of = by_channel[:].bitcast(BF16)
-        bk_c, gk_c, betak_c, mk_c, vk_c = [pair_of[:, HALVES * v : HALVES * (v + 1)] for v in range(1, 6)]
-        minus_half = keep.tile([P, HALVES], F32, name="minus_half")
-        nc.gpsimd.memset(minus_half[:], -0.5)
-        scale = keep.tile([P, HALVES], F32, name="scale")
-        shift = keep.tile([P, HALVES], F32, name="shift")
-        nc.gpsimd.tensor_scalar_add(out=scale[:], in0=vk_c, scalar1=EPS)
-        nc.gpsimd.tensor_tensor(out=scale[:], in0=scale[:], in1=minus_half[:], op=ALU.pow)
-        nc.gpsimd.tensor_mul(out=scale[:], in0=scale[:], in1=gk_c)
-        nc.gpsimd.tensor_sub(out=shift[:], in0=bk_c, in1=mk_c)
-        nc.gpsimd.tensor_mul(out=shift[:], in0=shift[:], in1=scale[:])
-        nc.gpsimd.tensor_add(out=shift[:], in0=shift[:], in1=betak_c)
 
         value_sum = total.tile([P, BANK], F32, name="value_sum")
         grouped = []
@@ -329,54 +323,70 @@ def tile_apnb_pa_kernel(tc, feats, Wk, bk, gk, betak, mk, vk, Wv, bv, out_0, out
         on_vector = nc.vector.tensor_copy
         on_scalar = nc.scalar.copy
 
-        regroup(0, 0, on_vector)
-        regroup(1, 0, on_scalar)
         for r, copy in enumerate((on_vector, on_scalar)):
             group_weight(wk_grouped, flip_weight(wk_rows, r, key_banks, "keys"), r, copy)
+        regroup(0, 0, on_vector)
+        regroup(1, 0, on_scalar)
+        wk_codes, wk_scales = quantise_weight(wk_grouped, "wk")
+        by_channel = keep.tile([P, 6], F32, name="by_channel")
+        vector_bank = val_banks.tile([P, BANK], F32, name="vector_bank", tag="vals")
+        nc.tensor.transpose(vector_bank[:, 0:P], vectors[:].bitcast(F32), ident[:])
+        nc.scalar.copy(out=by_channel[:], in_=vector_bank[:, 0:6])
+        pair_of = by_channel[:].bitcast(BF16)
+        bk_c, gk_c, betak_c, mk_c, vk_c = [pair_of[:, HALVES * v : HALVES * (v + 1)] for v in range(1, 6)]
+        minus_half = keep.tile([P, HALVES], F32, name="minus_half")
+        nc.gpsimd.memset(minus_half[:], -0.5)
+        scale = keep.tile([P, HALVES], F32, name="scale")
+        shift = keep.tile([P, HALVES], F32, name="shift")
+        nc.gpsimd.tensor_scalar_add(out=scale[:], in0=vk_c, scalar1=EPS)
+        nc.gpsimd.tensor_tensor(out=scale[:], in0=scale[:], in1=minus_half[:], op=ALU.pow)
+        nc.gpsimd.tensor_mul(out=scale[:], in0=scale[:], in1=gk_c)
+        nc.gpsimd.tensor_sub(out=shift[:], in0=bk_c, in1=mk_c)
+        nc.gpsimd.tensor_mul(out=shift[:], in0=shift[:], in1=scale[:])
+        nc.gpsimd.tensor_add(out=shift[:], in0=shift[:], in1=betak_c)
         regroup(0, 1, on_vector)
         regroup(1, 1, on_scalar)
-        wk_codes, wk_scales = quantise_weight(wk_grouped, "wk")
-        quantise(0)
         for r in range(HALVES):
             group_weight(wv_grouped, flip_weight(wv_rows, r, val_banks, "vals"), r, on_scalar)
+        quantise(0)
         project_keys(0)
-        regroup(2, 0, on_vector)
         quantise(1)
         project_keys(1)
-        leave_keys(0)
         wv_codes, wv_scales = quantise_weight(wv_grouped, "wv")
+        leave_keys(0)
         project_values(0)
-        project_values(1)
+        regroup(2, 0, on_vector)
         regroup(3, 0, on_scalar)
-        leave_values(0)
-        regroup(2, 1, on_vector)
-        leave_keys(1)
-        regroup(3, 1, on_scalar)
         pool_keys(0)
+        leave_values(0)
+        leave_keys(1)
+        project_values(1)
+        regroup(2, 1, on_vector)
+        regroup(3, 1, on_scalar)
+        pool_keys(1)
         quantise(2)
         leave_values(1)
         pool_values(0)
         project_keys(2)
         project_values(2)
-        regroup(4, 0, on_scalar)
-        pool_keys(1)
-        regroup(4, 1, on_vector)
         pool_values(1)
+        regroup(4, 0, on_scalar)
         quantise(3)
         project_keys(3)
         project_values(3)
+        regroup(4, 1, on_scalar)
         leave_keys(2)
         leave_values(2)
+        pool_keys(2)
         quantise(4)
         project_keys(4)
         project_values(4)
         pool_values(2)
+        pool_thirds(0)
+        pool_thirds(1)
         leave_keys(3)
         leave_values(3)
         pool_values(3)
-        pool_keys(2)
-        pool_thirds(0)
-        pool_thirds(1)
         pool_keys(3)
         leave_values(4)
         leave_keys(4)

@@ -205,6 +205,7 @@ def tile_apnb_pa_kernel(tc, feats, Wk, bk, gk, betak, mk, vk, Wv, bv, out_0, out
         kf_out = out_0.rearrange("b (p m) h w -> p (b m) (h w)", m=HALVES)
         pairs = keep.tile([P, HALVES, N // 2], F32, name="pairs")
         sums = keep.tile([P, HALVES, TOKENS], F32, name="sums")
+        unit_sums = keep.tile([P, HALVES, N_UNITS], F32, name="unit_sums")
         val_t = keep.tile([P, N_UNITS, CV], F32, name="val_t")
         key_bank = {}
         val_bank = {}
@@ -273,7 +274,12 @@ def tile_apnb_pa_kernel(tc, feats, Wk, bk, gk, betak, mk, vk, Wv, bv, out_0, out
                     out = out.rearrange("p (j e) -> p j e", e=2)
                     in_ = in_.rearrange("p (e j) -> p j e", e=2)
                 nc.scalar.activation(
-                    out=out, in_=in_, func=ACT.Relu, bias=shift[:, m : m + 1], scale=scale[:, m : m + 1]
+                    out=out,
+                    in_=in_,
+                    func=ACT.Relu,
+                    bias=shift[:, m : m + 1],
+                    scale=scale[:, m : m + 1],
+                    accum_out=unit_sums[:, m, i : i + 1],
                 )
             nc.sync.dma_start(out=kf_out[:, :, first : first + n], in_=kf[i][:])
 
@@ -323,11 +329,11 @@ def tile_apnb_pa_kernel(tc, feats, Wk, bk, gk, betak, mk, vk, Wv, bv, out_0, out
         on_vector = nc.vector.tensor_copy
         on_scalar = nc.scalar.copy
 
-        for r, copy in enumerate((on_vector, on_scalar)):
-            group_weight(wk_grouped, flip_weight(wk_rows, r, key_banks, "keys"), r, copy)
+        flips = [flip_weight(wk_rows, r, key_banks, "keys") for r in range(HALVES)]
+        group_weight(wk_grouped, flips[0], 0, on_vector)
         regroup(0, 0, on_vector)
         regroup(1, 0, on_scalar)
-        wk_codes, wk_scales = quantise_weight(wk_grouped, "wk")
+        group_weight(wk_grouped, flips[1], 1, on_scalar)
         by_channel = keep.tile([P, 6], F32, name="by_channel")
         vector_bank = val_banks.tile([P, BANK], F32, name="vector_bank", tag="vals")
         nc.tensor.transpose(vector_bank[:, 0:P], vectors[:].bitcast(F32), ident[:])
@@ -346,51 +352,52 @@ def tile_apnb_pa_kernel(tc, feats, Wk, bk, gk, betak, mk, vk, Wv, bv, out_0, out
         nc.gpsimd.tensor_add(out=shift[:], in0=shift[:], in1=betak_c)
         regroup(0, 1, on_vector)
         regroup(1, 1, on_scalar)
+        wk_codes, wk_scales = quantise_weight(wk_grouped, "wk")
+        quantise(0)
         for r in range(HALVES):
             group_weight(wv_grouped, flip_weight(wv_rows, r, val_banks, "vals"), r, on_scalar)
-        quantise(0)
-        project_keys(0)
         quantise(1)
+        project_keys(0)
         project_keys(1)
-        wv_codes, wv_scales = quantise_weight(wv_grouped, "wv")
         leave_keys(0)
-        project_values(0)
         regroup(2, 0, on_vector)
-        regroup(3, 0, on_scalar)
-        pool_keys(0)
-        leave_values(0)
-        leave_keys(1)
-        project_values(1)
+        regroup(3, 0, on_vector)
         regroup(2, 1, on_vector)
         regroup(3, 1, on_scalar)
-        pool_keys(1)
+        wv_codes, wv_scales = quantise_weight(wv_grouped, "wv")
+        project_values(0)
+        project_values(1)
         quantise(2)
-        leave_values(1)
-        pool_values(0)
         project_keys(2)
         project_values(2)
-        pool_values(1)
         regroup(4, 0, on_scalar)
+        leave_values(0)
+        leave_keys(1)
+        pool_keys(0)
         quantise(3)
         project_keys(3)
         project_values(3)
-        regroup(4, 1, on_scalar)
+        pool_values(0)
+        regroup(4, 1, on_vector)
+        leave_values(1)
         leave_keys(2)
-        leave_values(2)
-        pool_keys(2)
+        pool_values(1)
+        pool_keys(1)
         quantise(4)
         project_keys(4)
         project_values(4)
-        pool_values(2)
-        pool_thirds(0)
-        pool_thirds(1)
+        leave_values(2)
         leave_keys(3)
+        pool_values(2)
+        pool_keys(2)
         leave_values(3)
-        pool_values(3)
-        pool_keys(3)
         leave_values(4)
         leave_keys(4)
+        pool_values(3)
         pool_values(4)
+        pool_thirds(0)
+        pool_thirds(1)
+        pool_keys(3)
         pool_keys(4)
         pool_thirds(2)
 
@@ -398,7 +405,7 @@ def tile_apnb_pa_kernel(tc, feats, Wk, bk, gk, betak, mk, vk, Wv, bv, out_0, out
         nc.scalar.activation(out=value[:], in_=value_sum[:, 0:CV], func=ACT.Copy, scale=token_weight[:, 0:1])
         nc.sync.dma_start(out=out_2.rearrange("b t c -> (b t) c"), in_=value[0:TOKENS, :])
 
-        nc.vector.tensor_reduce(out=sums[:, :, 0:1], in_=sums[:, :, FIRST[3] : FIRST[6]], axis=AXIS.X, op=ALU.add)
+        nc.vector.tensor_reduce(out=sums[:, :, 0:1], in_=unit_sums[:], axis=AXIS.X, op=ALU.add)
         keyp = keep.tile([P, HALVES, TOKENS], F32, name="keyp")
         nc.vector.tensor_tensor(
             out=keyp[:],

@@ -51,20 +51,16 @@ def tile_apnb_pa_kernel(tc, feats, Wk, bk, gk, betak, mk, vk, Wv, bv, out_0, out
         total = ctx.enter_context(tc.psum_pool(name="total", bufs=1))
         ctx.enter_context(tc.manual_schedule())
 
-        vectors = keep.tile([P, CV], BF16, name="vectors")
-        nc.vector.memset(vectors[:], 0.0)
-
-        def load_vectors(queue, first_row, values):
-            for row, value in enumerate(values):
-                queue.dma_start(
-                    out=vectors[first_row + row : first_row + row + 1, :], in_=value.rearrange("(o c) -> o c", o=1)
-                )
+        by_channel = keep.tile([P, 5, 16], BF16, name="by_channel")
+        for v, values in enumerate((vk, gk, bk, mk, betak)):
+            nc.scalar.dma_start(out=by_channel[:, v, 0:HALVES], in_=values.rearrange("(p m) -> p m", m=HALVES))
+        bv_row = keep.tile([P, CV], BF16, name="bv_row")
+        nc.gpsimd.memset(bv_row[:], 0.0)
 
         place_of = keep.tile([P, N_UNITS], I32, name="place_of")
         nc.gpsimd.iota(place_of[:, 0 : N_UNITS - 1], pattern=[[2 * P, N_UNITS - 1]], base=0, channel_multiplier=2)
         nc.gpsimd.iota(place_of[:, N_UNITS - 1 : N_UNITS], pattern=[[0, 1]], base=UNITS[-1][0], channel_multiplier=1)
 
-        load_vectors(nc.scalar, 0, (bv, bk, gk, betak))
 
         x_rows = feats.rearrange("b (g q t) h w -> q (b g) t (h w)", g=PASSES, t=PACK)
         raw = [keep.tile([P, PASSES, PACK, n], BF16, name="raw%d" % i) for i, (first, n) in enumerate(LOADS)]
@@ -81,12 +77,12 @@ def tile_apnb_pa_kernel(tc, feats, Wk, bk, gk, betak, mk, vk, Wv, bv, out_0, out
         wk_rows = load_weight(Wk.rearrange("(p r) k -> p r k", r=HALVES), "wk_rows")
         for g in range(PASSES):
             load_feats(0, g)
-        load_vectors(nc.sync, 4, (mk, vk))
         wv_rows = load_weight(Wv.rearrange("(r p) k -> p r k", p=P), "wv_rows")
         load_feats(1, 0)
         load_feats(1, 1)
         for g in range(PASSES):
             load_feats(2, g)
+        nc.sync.dma_start(out=bv_row[0:1, :], in_=bv.rearrange("(o c) -> o c", o=1))
 
         warm = keep.tile([P, 1], F32, name="warm")
         nc.vector.memset(warm[:], 0.0)
@@ -101,6 +97,18 @@ def tile_apnb_pa_kernel(tc, feats, Wk, bk, gk, betak, mk, vk, Wv, bv, out_0, out
         nc.gpsimd.memset(bias_pick[:], 0.0)
         for s in LEVELS:
             nc.gpsimd.memset(bias_pick[0:1, FIRST[s] : FIRST[s] + s * s], float(N // (s * s)))
+
+        vk_c, gk_c, bk_c, mk_c, betak_c = [by_channel[:, v, 0:HALVES] for v in range(5)]
+        minus_half = keep.tile([P, HALVES], F32, name="minus_half")
+        nc.gpsimd.memset(minus_half[:], -0.5)
+        scale = keep.tile([P, HALVES], F32, name="scale")
+        shift = keep.tile([P, HALVES], F32, name="shift")
+        nc.gpsimd.tensor_scalar_add(out=scale[:], in0=vk_c, scalar1=EPS)
+        nc.gpsimd.tensor_tensor(out=scale[:], in0=scale[:], in1=minus_half[:], op=ALU.pow)
+        nc.gpsimd.tensor_mul(out=scale[:], in0=scale[:], in1=gk_c)
+        nc.gpsimd.tensor_sub(out=shift[:], in0=bk_c, in1=mk_c)
+        nc.gpsimd.tensor_mul(out=shift[:], in0=shift[:], in1=scale[:])
+        nc.gpsimd.tensor_add(out=shift[:], in0=shift[:], in1=betak_c)
 
         product = keep.tile([P, 2, N_UNITS], I32, name="product")
         place = keep.tile([P, 2, N_UNITS], I32, name="place")
@@ -144,7 +152,7 @@ def tile_apnb_pa_kernel(tc, feats, Wk, bk, gk, betak, mk, vk, Wv, bv, out_0, out
 
         weight = keep.tile([P, TOKENS], F32, name="weight")
         for s in LEVELS:
-            nc.vector.tensor_scalar(
+            nc.gpsimd.tensor_scalar(
                 out=weight[:, FIRST[s] : FIRST[s] + s * s],
                 in0=count[:, 0 : s * s],
                 scalar1=0.0,
@@ -152,17 +160,6 @@ def tile_apnb_pa_kernel(tc, feats, Wk, bk, gk, betak, mk, vk, Wv, bv, out_0, out
                 op0=ALU.mult,
                 op1=ALU.add,
             )
-        token_weight = keep.tile([P, 1], F32, name="token_weight")
-        diagonal = keep.tile([P, TOKENS], F32, name="diagonal")
-        nc.vector.scalar_tensor_tensor(
-            out=diagonal[:],
-            in0=ident[:, 0:TOKENS],
-            scalar=1.0,
-            in1=weight[:],
-            op0=ALU.mult,
-            op1=ALU.mult,
-            accum_out=token_weight[:],
-        )
 
         def flip_weight(rows, r, psum, tag):
             words = rows[:, r, :].bitcast(F32)
@@ -203,7 +200,7 @@ def tile_apnb_pa_kernel(tc, feats, Wk, bk, gk, betak, mk, vk, Wv, bv, out_0, out
             x_scales.append(keep.tile([P, PASSES, n], U8, name="x_scales%d" % i, align_bytes=64))
         kf = [keep.tile([P, HALVES, n], F32, name="kf%d" % i) for i, (first, n) in enumerate(UNITS)]
         kf_out = out_0.rearrange("b (p m) h w -> p (b m) (h w)", m=HALVES)
-        pairs = keep.tile([P, HALVES, N // 2], F32, name="pairs")
+        pairs = keep.tile([P, N // 2, HALVES], F32, name="pairs")
         sums = keep.tile([P, HALVES, TOKENS], F32, name="sums")
         unit_sums = keep.tile([P, HALVES, N_UNITS], F32, name="unit_sums")
         val_t = keep.tile([P, N_UNITS, CV], F32, name="val_t")
@@ -285,33 +282,36 @@ def tile_apnb_pa_kernel(tc, feats, Wk, bk, gk, betak, mk, vk, Wv, bv, out_0, out
 
         def pool_values(i):
             if i == 0:
-                nc.tensor.matmul(out=value_sum[:, 0:CV], lhsT=bias_pick[:], rhs=vectors[:], start=True, stop=False)
+                nc.tensor.matmul(out=value_sum[:, 0:CV], lhsT=bias_pick[:], rhs=bv_row[:], start=True, stop=False)
             nc.tensor.matmul(
                 out=value_sum[:, 0:CV], lhsT=pool[:, i, :], rhs=val_t[:, i, :], start=False, stop=(i == N_UNITS - 1)
             )
 
-        def pool_keys(i):
+        def pair_keys(i):
             first, n = UNITS[i]
-            two = kf[i][:].rearrange("p m (q e) -> p m q e", e=2)
-            nc.vector.tensor_tensor(
-                out=pairs[:, :, first // 2 : (first + n) // 2], in0=two[:, :, :, 0], in1=two[:, :, :, 1], op=ALU.add
+            two = kf[i][:].rearrange("p m (q e) -> p q e m", e=2)
+            adder = nc.vector if i == N_UNITS - 1 else nc.gpsimd
+            adder.tensor_tensor(
+                out=pairs[:, first // 2 : (first + n) // 2, :], in0=two[:, :, 0, :], in1=two[:, :, 1, :], op=ALU.add
             )
+
+        def pool_keys(i):
             for s, b0, b1 in BANDS_AFTER[i]:
                 pool_bands(s, b0, b1)
 
         def pool_bands(s, b0, b1):
             half_band = H // s * W // 2
             out = sums[:, :, FIRST[s] + b0 * s : FIRST[s] + b1 * s]
-            in_ = pairs[:, :, b0 * half_band : b1 * half_band]
+            in_ = pairs[:, b0 * half_band : b1 * half_band, :]
             if b1 - b0 == 1:
                 nc.vector.tensor_reduce(
-                    out=out, in_=in_.rearrange("p m (r c x) -> p m c r x", r=H // s, c=s), axis=AXIS.XY, op=ALU.add
+                    out=out, in_=in_.rearrange("p (r c x) m -> p m c r x", r=H // s, c=s), axis=AXIS.XY, op=ALU.add
                 )
             else:
                 for m in range(HALVES):
                     nc.vector.tensor_reduce(
                         out=out[:, m, :].rearrange("p (b c) -> p b c", c=s),
-                        in_=in_[:, m, :].rearrange("p (b r c x) -> p b c r x", b=b1 - b0, r=H // s, c=s),
+                        in_=in_[:, :, m].rearrange("p (b r c x) -> p b c r x", b=b1 - b0, r=H // s, c=s),
                         axis=AXIS.XY,
                         op=ALU.add,
                     )
@@ -329,75 +329,81 @@ def tile_apnb_pa_kernel(tc, feats, Wk, bk, gk, betak, mk, vk, Wv, bv, out_0, out
         on_vector = nc.vector.tensor_copy
         on_scalar = nc.scalar.copy
 
+        def keep_busy(times):
+            for i in range(times):
+                nc.tensor.matmul(out=value_sum[:, 0:P], lhsT=ident[:], rhs=ident[:], start=True, stop=True)
+
+        keep_busy(3)
         flips = [flip_weight(wk_rows, r, key_banks, "keys") for r in range(HALVES)]
         group_weight(wk_grouped, flips[0], 0, on_vector)
         regroup(0, 0, on_vector)
         regroup(1, 0, on_scalar)
         group_weight(wk_grouped, flips[1], 1, on_scalar)
-        by_channel = keep.tile([P, 6], F32, name="by_channel")
-        vector_bank = val_banks.tile([P, BANK], F32, name="vector_bank", tag="vals")
-        nc.tensor.transpose(vector_bank[:, 0:P], vectors[:].bitcast(F32), ident[:])
-        nc.scalar.copy(out=by_channel[:], in_=vector_bank[:, 0:6])
-        pair_of = by_channel[:].bitcast(BF16)
-        bk_c, gk_c, betak_c, mk_c, vk_c = [pair_of[:, HALVES * v : HALVES * (v + 1)] for v in range(1, 6)]
-        minus_half = keep.tile([P, HALVES], F32, name="minus_half")
-        nc.gpsimd.memset(minus_half[:], -0.5)
-        scale = keep.tile([P, HALVES], F32, name="scale")
-        shift = keep.tile([P, HALVES], F32, name="shift")
-        nc.gpsimd.tensor_scalar_add(out=scale[:], in0=vk_c, scalar1=EPS)
-        nc.gpsimd.tensor_tensor(out=scale[:], in0=scale[:], in1=minus_half[:], op=ALU.pow)
-        nc.gpsimd.tensor_mul(out=scale[:], in0=scale[:], in1=gk_c)
-        nc.gpsimd.tensor_sub(out=shift[:], in0=bk_c, in1=mk_c)
-        nc.gpsimd.tensor_mul(out=shift[:], in0=shift[:], in1=scale[:])
-        nc.gpsimd.tensor_add(out=shift[:], in0=shift[:], in1=betak_c)
         regroup(0, 1, on_vector)
         regroup(1, 1, on_scalar)
         wk_codes, wk_scales = quantise_weight(wk_grouped, "wk")
         quantise(0)
-        for r in range(HALVES):
-            group_weight(wv_grouped, flip_weight(wv_rows, r, val_banks, "vals"), r, on_scalar)
+        keep_busy(4)
+        flips = [flip_weight(wv_rows, r, val_banks, "vals") for r in range(HALVES)]
+        group_weight(wv_grouped, flips[0], 0, on_scalar)
+        group_weight(wv_grouped, flips[1], 1, on_scalar)
         quantise(1)
         project_keys(0)
         project_keys(1)
-        leave_keys(0)
         regroup(2, 0, on_vector)
-        regroup(3, 0, on_vector)
-        regroup(2, 1, on_vector)
-        regroup(3, 1, on_scalar)
         wv_codes, wv_scales = quantise_weight(wv_grouped, "wv")
+        leave_keys(0)
+        pair_keys(0)
+        regroup(3, 0, on_scalar)
         project_values(0)
         project_values(1)
+        leave_values(0)
+        pool_values(0)
+        regroup(2, 1, on_vector)
+        regroup(3, 1, on_vector)
         quantise(2)
+        leave_values(1)
+        leave_keys(1)
+        pair_keys(1)
         project_keys(2)
         project_values(2)
-        regroup(4, 0, on_scalar)
-        leave_values(0)
-        leave_keys(1)
-        pool_keys(0)
+        pool_values(1)
+        regroup(4, 0, on_vector)
+        regroup(4, 1, on_vector)
         quantise(3)
         project_keys(3)
         project_values(3)
-        pool_values(0)
-        regroup(4, 1, on_vector)
-        leave_values(1)
         leave_keys(2)
-        pool_values(1)
-        pool_keys(1)
+        pair_keys(2)
         quantise(4)
+        leave_values(2)
         project_keys(4)
         project_values(4)
-        leave_values(2)
-        leave_keys(3)
         pool_values(2)
-        pool_keys(2)
+        pool_keys(1)
+        leave_keys(3)
+        pair_keys(3)
         leave_values(3)
-        leave_values(4)
-        leave_keys(4)
         pool_values(3)
-        pool_values(4)
+        leave_keys(4)
+        pool_keys(2)
         pool_thirds(0)
         pool_thirds(1)
+        leave_values(4)
+        pool_values(4)
+        token_weight = keep.tile([P, 1], F32, name="token_weight")
+        diagonal = keep.tile([P, TOKENS], F32, name="diagonal")
+        nc.vector.scalar_tensor_tensor(
+            out=diagonal[:],
+            in0=ident[:, 0:TOKENS],
+            scalar=1.0,
+            in1=weight[:],
+            op0=ALU.mult,
+            op1=ALU.mult,
+            accum_out=token_weight[:],
+        )
         pool_keys(3)
+        pair_keys(4)
         pool_keys(4)
         pool_thirds(2)
 

@@ -290,7 +290,7 @@ def tile_apnb_pa_kernel(tc, feats, Wk, bk, gk, betak, mk, vk, Wv, bv, out_0, out
         def pair_keys(i):
             first, n = UNITS[i]
             two = kf[i][:].rearrange("p m (q e) -> p q e m", e=2)
-            adder = nc.vector if i == N_UNITS - 1 else nc.gpsimd
+            adder = nc.gpsimd if i < 3 else nc.vector
             adder.tensor_tensor(
                 out=pairs[:, first // 2 : (first + n) // 2, :], in0=two[:, :, 0, :], in1=two[:, :, 1, :], op=ALU.add
             )
@@ -329,21 +329,34 @@ def tile_apnb_pa_kernel(tc, feats, Wk, bk, gk, betak, mk, vk, Wv, bv, out_0, out
         on_vector = nc.vector.tensor_copy
         on_scalar = nc.scalar.copy
 
-        def keep_busy(times):
+        def keep_awake(times):
             for i in range(times):
                 nc.tensor.matmul(out=value_sum[:, 0:P], lhsT=ident[:], rhs=ident[:], start=True, stop=True)
 
-        keep_busy(3)
+        def keep_awake_by_codes(times):
+            for i in range(times):
+                nc.tensor.matmul_mx(
+                    out=value_sum[:, 0:CK],
+                    lhsT=wk_codes[:, 0, 0:P].bitcast(FP8X4),
+                    lhsT_scale=wk_scales[:, 0, 0:P],
+                    rhs=wk_codes[:, 0, :].bitcast(FP8X4),
+                    rhs_scale=wk_scales[:, 0, :],
+                    start=True,
+                    stop=True,
+                )
+
+        keep_awake(3)
         flips = [flip_weight(wk_rows, r, key_banks, "keys") for r in range(HALVES)]
+        keep_awake(4)
         group_weight(wk_grouped, flips[0], 0, on_vector)
         regroup(0, 0, on_vector)
-        regroup(1, 0, on_scalar)
         group_weight(wk_grouped, flips[1], 1, on_scalar)
+        regroup(1, 0, on_scalar)
+        wk_codes, wk_scales = quantise_weight(wk_grouped, "wk")
+        keep_awake_by_codes(5)
         regroup(0, 1, on_vector)
         regroup(1, 1, on_scalar)
-        wk_codes, wk_scales = quantise_weight(wk_grouped, "wk")
         quantise(0)
-        keep_busy(4)
         flips = [flip_weight(wv_rows, r, val_banks, "vals") for r in range(HALVES)]
         group_weight(wv_grouped, flips[0], 0, on_scalar)
         group_weight(wv_grouped, flips[1], 1, on_scalar)
@@ -351,6 +364,17 @@ def tile_apnb_pa_kernel(tc, feats, Wk, bk, gk, betak, mk, vk, Wv, bv, out_0, out
         project_keys(0)
         project_keys(1)
         regroup(2, 0, on_vector)
+        token_weight = keep.tile([P, 1], F32, name="token_weight")
+        diagonal = keep.tile([P, TOKENS], F32, name="diagonal")
+        nc.vector.scalar_tensor_tensor(
+            out=diagonal[:],
+            in0=ident[:, 0:TOKENS],
+            scalar=1.0,
+            in1=weight[:],
+            op0=ALU.mult,
+            op1=ALU.mult,
+            accum_out=token_weight[:],
+        )
         wv_codes, wv_scales = quantise_weight(wv_grouped, "wv")
         leave_keys(0)
         pair_keys(0)
@@ -391,17 +415,6 @@ def tile_apnb_pa_kernel(tc, feats, Wk, bk, gk, betak, mk, vk, Wv, bv, out_0, out
         pool_thirds(1)
         leave_values(4)
         pool_values(4)
-        token_weight = keep.tile([P, 1], F32, name="token_weight")
-        diagonal = keep.tile([P, TOKENS], F32, name="diagonal")
-        nc.vector.scalar_tensor_tensor(
-            out=diagonal[:],
-            in0=ident[:, 0:TOKENS],
-            scalar=1.0,
-            in1=weight[:],
-            op0=ALU.mult,
-            op1=ALU.mult,
-            accum_out=token_weight[:],
-        )
         pool_keys(3)
         pair_keys(4)
         pool_keys(4)

@@ -33,7 +33,7 @@ N_UNITS = len(UNITS)
 LOADS = ((0, 512), (512, 512), (1024, 128))
 LOAD_OF = (0, 0, 1, 1, 2)
 
-BANDS_AFTER = ((), ((8, 0, 3), (6, 0, 2)), ((8, 3, 5), (6, 2, 4)), ((8, 5, 7), (6, 4, 5)), ((6, 5, 6), (8, 7, 8)))
+BANDS_AFTER = (((8, 0, 1), (6, 0, 1)), ((8, 1, 3), (6, 1, 2)), ((8, 3, 5), (6, 2, 4)), ((8, 5, 7), (6, 4, 5)), ((6, 5, 6), (8, 7, 8)))
 
 LEVELS = (1, 3, 6, 8)
 FIRST = {1: 0, 3: 1, 6: 10, 8: 46}
@@ -52,8 +52,12 @@ def tile_apnb_pa_kernel(tc, feats, Wk, bk, gk, betak, mk, vk, Wv, bv, out_0, out
         ctx.enter_context(tc.manual_schedule())
 
         by_channel = keep.tile([P, 5, 16], BF16, name="by_channel")
-        for v, values in enumerate((vk, gk, bk, mk, betak)):
-            nc.scalar.dma_start(out=by_channel[:, v, 0:HALVES], in_=values.rearrange("(p m) -> p m", m=HALVES))
+
+        def load_by_channel(queue, v, values):
+            queue.dma_start(out=by_channel[:, v, 0:HALVES], in_=values.rearrange("(p m) -> p m", m=HALVES))
+
+        for v, values in enumerate((vk, gk, bk, mk)):
+            load_by_channel(nc.scalar, v, values)
         bv_row = keep.tile([P, CV], BF16, name="bv_row")
         nc.gpsimd.memset(bv_row[:], 0.0)
 
@@ -78,15 +82,16 @@ def tile_apnb_pa_kernel(tc, feats, Wk, bk, gk, betak, mk, vk, Wv, bv, out_0, out
         for g in range(PASSES):
             load_feats(0, g)
         wv_rows = load_weight(Wv.rearrange("(r p) k -> p r k", p=P), "wv_rows")
+        nc.sync.dma_start(out=bv_row[0:1, :], in_=bv.rearrange("(o c) -> o c", o=1))
         load_feats(1, 0)
         load_feats(1, 1)
         for g in range(PASSES):
             load_feats(2, g)
-        nc.sync.dma_start(out=bv_row[0:1, :], in_=bv.rearrange("(o c) -> o c", o=1))
 
         warm = keep.tile([P, 1], F32, name="warm")
         nc.vector.memset(warm[:], 0.0)
         nc.scalar.activation(out=warm[:], in_=warm[:], func=ACT.Relu)
+        load_by_channel(nc.scalar, 4, betak)
         count = keep.tile([P, 64], F32, name="count")
         nc.gpsimd.iota(
             count[:], pattern=[[1, 64]], base=0, channel_multiplier=0, allow_small_or_imprecise_dtypes=True
@@ -280,9 +285,10 @@ def tile_apnb_pa_kernel(tc, feats, Wk, bk, gk, betak, mk, vk, Wv, bv, out_0, out
                 )
             nc.sync.dma_start(out=kf_out[:, :, first : first + n], in_=kf[i][:])
 
+        def begin_values():
+            nc.tensor.matmul(out=value_sum[:, 0:CV], lhsT=bias_pick[:], rhs=bv_row[:], start=True, stop=False)
+
         def pool_values(i):
-            if i == 0:
-                nc.tensor.matmul(out=value_sum[:, 0:CV], lhsT=bias_pick[:], rhs=bv_row[:], start=True, stop=False)
             nc.tensor.matmul(
                 out=value_sum[:, 0:CV], lhsT=pool[:, i, :], rhs=val_t[:, i, :], start=False, stop=(i == N_UNITS - 1)
             )
@@ -290,7 +296,7 @@ def tile_apnb_pa_kernel(tc, feats, Wk, bk, gk, betak, mk, vk, Wv, bv, out_0, out
         def pair_keys(i):
             first, n = UNITS[i]
             two = kf[i][:].rearrange("p m (q e) -> p q e m", e=2)
-            adder = nc.gpsimd if i < 3 else nc.vector
+            adder = nc.gpsimd if i < 2 else nc.vector
             adder.tensor_tensor(
                 out=pairs[:, first // 2 : (first + n) // 2, :], in0=two[:, :, 0, :], in1=two[:, :, 1, :], op=ALU.add
             )
@@ -379,6 +385,7 @@ def tile_apnb_pa_kernel(tc, feats, Wk, bk, gk, betak, mk, vk, Wv, bv, out_0, out
         leave_keys(0)
         pair_keys(0)
         regroup(3, 0, on_scalar)
+        begin_values()
         project_values(0)
         project_values(1)
         leave_values(0)
@@ -386,9 +393,9 @@ def tile_apnb_pa_kernel(tc, feats, Wk, bk, gk, betak, mk, vk, Wv, bv, out_0, out
         regroup(2, 1, on_vector)
         regroup(3, 1, on_vector)
         quantise(2)
-        leave_values(1)
         leave_keys(1)
         pair_keys(1)
+        leave_values(1)
         project_keys(2)
         project_values(2)
         pool_values(1)
@@ -398,21 +405,22 @@ def tile_apnb_pa_kernel(tc, feats, Wk, bk, gk, betak, mk, vk, Wv, bv, out_0, out
         project_keys(3)
         project_values(3)
         leave_keys(2)
-        pair_keys(2)
         quantise(4)
         leave_values(2)
         project_keys(4)
         project_values(4)
         pool_values(2)
+        pool_keys(0)
         pool_keys(1)
+        pair_keys(2)
         leave_keys(3)
-        pair_keys(3)
         leave_values(3)
         pool_values(3)
         leave_keys(4)
         pool_keys(2)
         pool_thirds(0)
         pool_thirds(1)
+        pair_keys(3)
         leave_values(4)
         pool_values(4)
         pool_keys(3)
@@ -422,7 +430,11 @@ def tile_apnb_pa_kernel(tc, feats, Wk, bk, gk, betak, mk, vk, Wv, bv, out_0, out
 
         value = keep.tile([P, CV], F32, name="value")
         nc.scalar.activation(out=value[:], in_=value_sum[:, 0:CV], func=ACT.Copy, scale=token_weight[:, 0:1])
-        nc.sync.dma_start(out=out_2.rearrange("b t c -> (b t) c"), in_=value[0:TOKENS, :])
+        value_out = out_2.rearrange("b t c -> (b t) c")
+        done = 0
+        for n in (64, 32, 8, 4, 2):
+            nc.scalar.dma_start(out=value_out[done : done + n, :], in_=value[done : done + n, :])
+            done += n
 
         nc.vector.tensor_reduce(out=sums[:, :, 0:1], in_=unit_sums[:], axis=AXIS.X, op=ALU.add)
         keyp = keep.tile([P, HALVES, TOKENS], F32, name="keyp")

from contextlib import ExitStack

import concourse.mybir as mybir
from concourse.masks import make_identity

F32 = mybir.dt.float32
BF16 = mybir.dt.bfloat16
I32 = mybir.dt.int32
U32 = mybir.dt.uint32
U8 = mybir.dt.uint8
FP8X4 = mybir.dt.float8_e4m3fn_x4
ALU = mybir.AluOpType
ACT = mybir.ActivationFunctionType
AXIS = mybir.AxisListType

P = 128
PACK = 4
K_PASS = P * PACK
BANK = 512

C = 1024
PASSES = C // K_PASS
CK = 256
CV = 256
HALVES = CK // P
H = 24
W = 48
N = H * W
EPS = 1e-5

UNITS = ((0, 256), (256, 256), (512, 256), (768, 256), (1024, 128))
N_UNITS = len(UNITS)
LOADS = ((0, 512), (512, 512), (1024, 128))
LOAD_OF = (0, 0, 1, 1, 2)

BANDS_AFTER = (((8, 0, 1), (6, 0, 1)), ((8, 1, 3), (6, 1, 2)), ((8, 3, 5), (6, 2, 4)), ((8, 5, 7), (6, 4, 5)), ((6, 5, 6), (8, 7, 8)))

LEVELS = (1, 3, 6, 8)
FIRST = {1: 0, 3: 1, 6: 10, 8: 46}
TOKENS = 110

FLOPS = 2 * (CK + CV) * C * N


def tile_apnb_pa_kernel(tc, feats, Wk, bk, gk, betak, mk, vk, Wv, bv, out_0, out_1, out_2):
    nc = tc.nc
    with ExitStack() as ctx:
        keep = ctx.enter_context(tc.tile_pool(name="keep", bufs=1))
        key_banks = ctx.enter_context(tc.psum_pool(name="key_banks", bufs=4))
        val_banks = ctx.enter_context(tc.psum_pool(name="val_banks", bufs=3))
        total = ctx.enter_context(tc.psum_pool(name="total", bufs=1))
        ctx.enter_context(tc.manual_schedule())

        by_channel = keep.tile([P, 5, 16], BF16, name="by_channel")

        def load_by_channel(queue, v, values):
            queue.dma_start(out=by_channel[:, v, 0:HALVES], in_=values.rearrange("(p m) -> p m", m=HALVES))

        for v, values in enumerate((vk, gk, bk, mk)):
            load_by_channel(nc.scalar, v, values)
        bv_row = keep.tile([P, CV], BF16, name="bv_row")
        nc.gpsimd.memset(bv_row[:], 0.0)

        place_of = keep.tile([P, N_UNITS], I32, name="place_of")
        nc.gpsimd.iota(place_of[:, 0 : N_UNITS - 1], pattern=[[2 * P, N_UNITS - 1]], base=0, channel_multiplier=2)
        nc.gpsimd.iota(place_of[:, N_UNITS - 1 : N_UNITS], pattern=[[0, 1]], base=UNITS[-1][0], channel_multiplier=1)


        x_rows = feats.rearrange("b (g q t) h w -> q (b g) t (h w)", g=PASSES, t=PACK)
        raw = [keep.tile([P, PASSES, PACK, n], BF16, name="raw%d" % i) for i, (first, n) in enumerate(LOADS)]

        def load_feats(i, g):
            first, n = LOADS[i]
            nc.sync.dma_start(out=raw[i][:, g], in_=x_rows[:, g, :, first : first + n])

        def load_weight(rows_by_partition, name):
            rows = keep.tile([P, HALVES, C], BF16, name=name)
            nc.sync.dma_start(out=rows[:], in_=rows_by_partition)
            return rows

        wk_rows = load_weight(Wk.rearrange("(p r) k -> p r k", r=HALVES), "wk_rows")
        for g in range(PASSES):
            load_feats(0, g)
        wv_rows = load_weight(Wv.rearrange("(r p) k -> p r k", p=P), "wv_rows")
        nc.sync.dma_start(out=bv_row[0:1, :], in_=bv.rearrange("(o c) -> o c", o=1))
        load_feats(1, 0)
        load_feats(1, 1)
        for g in range(PASSES):
            load_feats(2, g)

        warm = keep.tile([P, 1], F32, name="warm")
        nc.vector.memset(warm[:], 0.0)
        nc.scalar.activation(out=warm[:], in_=warm[:], func=ACT.Relu)
        load_by_channel(nc.scalar, 4, betak)
        count = keep.tile([P, 64], F32, name="count")
        nc.gpsimd.iota(
            count[:], pattern=[[1, 64]], base=0, channel_multiplier=0, allow_small_or_imprecise_dtypes=True
        )
        ident = keep.tile([P, P], F32, name="ident")
        make_identity(nc, ident[:])
        bias_pick = keep.tile([P, P], BF16, name="bias_pick")
        nc.gpsimd.memset(bias_pick[:], 0.0)
        for s in LEVELS:
            nc.gpsimd.memset(bias_pick[0:1, FIRST[s] : FIRST[s] + s * s], float(N // (s * s)))

        vk_c, gk_c, bk_c, mk_c, betak_c = [by_channel[:, v, 0:HALVES] for v in range(5)]
        minus_half = keep.tile([P, HALVES], F32, name="minus_half")
        nc.gpsimd.memset(minus_half[:], -0.5)
        scale = keep.tile([P, HALVES], F32, name="scale")
        shift = keep.tile([P, HALVES], F32, name="shift")
        nc.gpsimd.tensor_scalar_add(out=scale[:], in0=vk_c, scalar1=EPS)
        nc.gpsimd.tensor_tensor(out=scale[:], in0=scale[:], in1=minus_half[:], op=ALU.pow)
        nc.gpsimd.tensor_mul(out=scale[:], in0=scale[:], in1=gk_c)
        nc.gpsimd.tensor_sub(out=shift[:], in0=bk_c, in1=mk_c)
        nc.gpsimd.tensor_mul(out=shift[:], in0=shift[:], in1=scale[:])
        nc.gpsimd.tensor_add(out=shift[:], in0=shift[:], in1=betak_c)

        product = keep.tile([P, 2, N_UNITS], I32, name="product")
        place = keep.tile([P, 2, N_UNITS], I32, name="place")
        nc.vector.tensor_scalar(out=product[:, 0, :], in0=place_of[:], scalar1=1366.0, scalar2=None, op0=ALU.mult)
        nc.vector.tensor_scalar(
            out=place[:, 0, :],
            in0=product[:, 0, :],
            scalar1=16,
            scalar2=1,
            op0=ALU.logical_shift_right,
            op1=ALU.logical_shift_left,
        )
        nc.vector.scalar_tensor_tensor(
            out=place[:, 1, :], in0=place[:, 0, :], scalar=-24.0, in1=place_of[:], op0=ALU.mult, op1=ALU.add
        )
        band_cell = keep.tile([P, 3, 2, N_UNITS], I32, name="band_cell")
        nc.vector.tensor_scalar(out=product[:], in0=place[:], scalar1=683.0, scalar2=None, op0=ALU.mult)
        nc.vector.tensor_scalar(out=band_cell[:, 0], in0=place[:], scalar1=4, scalar2=None, op0=ALU.logical_shift_right)
        nc.vector.tensor_scalar(out=band_cell[:, 1], in0=place[:], scalar1=3, scalar2=None, op0=ALU.logical_shift_right)
        nc.vector.tensor_scalar(out=band_cell[:, 2], in0=product[:], scalar1=12, scalar2=None, op0=ALU.logical_shift_right)
        cell = keep.tile([P, 3, N_UNITS], F32, name="cell")
        pool = keep.tile([P, N_UNITS, P], F32, name="pool")
        nc.vector.memset(pool[:, :, 0:1], 1.0)
        nc.vector.memset(pool[:, :, TOKENS:P], 0.0)
        for l, s in enumerate(LEVELS[1:]):
            nc.vector.scalar_tensor_tensor(
                out=cell[:, l, :],
                in0=band_cell[:, l, 0, :],
                scalar=float(s),
                in1=band_cell[:, l, 1, :],
                op0=ALU.mult,
                op1=ALU.add,
            )
            shape = [P, N_UNITS, s * s]
            nc.vector.tensor_tensor(
                out=pool[:, :, FIRST[s] : FIRST[s] + s * s],
                in0=count[:, 0 : s * s].unsqueeze(1).to_broadcast(shape),
                in1=cell[:, l, :].unsqueeze(2).to_broadcast(shape),
                op=ALU.is_equal,
            )

        weight = keep.tile([P, TOKENS], F32, name="weight")
        for s in LEVELS:
            nc.gpsimd.tensor_scalar(
                out=weight[:, FIRST[s] : FIRST[s] + s * s],
                in0=count[:, 0 : s * s],
                scalar1=0.0,
                scalar2=float(s * s) / N,
                op0=ALU.mult,
                op1=ALU.add,
            )

        def flip_weight(rows, r, psum, tag):
            words = rows[:, r, :].bitcast(F32)
            bank = psum.tile([P, BANK], F32, name="flip_bank", tag=tag)
            for g in range(PASSES):
                for u in range(2):
                    s = 2 * g + u
                    every_second = words[:, 2 * P * g + u : 2 * P * (g + 1) : 2]
                    nc.tensor.transpose(bank[:, s * P : (s + 1) * P], every_second, ident[:])
            return bank

        def group_weight(w_grouped, bank, r, copy):
            copy(
                out=w_grouped[:].bitcast(F32)[:, :, r * P : (r + 1) * P, :],
                in_=bank[:].rearrange("p (g u o) -> p g o u", g=PASSES, u=2),
            )

        def quantise_weight(w_grouped, name):
            codes = keep.tile([P, PASSES, HALVES * P], U32, name=name + "_codes", align_bytes=64)
            scales = keep.tile([P, PASSES, HALVES * P], U8, name=name + "_scales", align_bytes=64)
            nc.vector.quantize_mx(
                out=codes[:].rearrange("p g o -> p (g o)").bitcast(FP8X4),
                scales=scales[:].rearrange("p g o -> p (g o)"),
                in_=w_grouped[:].rearrange("p g o t -> p (g o t)"),
            )
            return codes, scales

        wk_grouped = keep.tile([P, PASSES, HALVES * P, PACK], BF16, name="wk_grouped", align_bytes=64)
        wv_grouped = keep.tile([P, PASSES, HALVES * P, PACK], BF16, name="wv_grouped", align_bytes=64)

        value_sum = total.tile([P, BANK], F32, name="value_sum")
        grouped = []
        x_codes = []
        x_scales = []
        for i, (first, n) in enumerate(UNITS):
            grouped.append(keep.tile([P, PASSES, n, PACK], BF16, name="grouped%d" % i, align_bytes=64))
            x_codes.append(keep.tile([P, PASSES, n], U32, name="x_codes%d" % i, align_bytes=64))
            x_scales.append(keep.tile([P, PASSES, n], U8, name="x_scales%d" % i, align_bytes=64))
        kf = [keep.tile([P, HALVES, n], F32, name="kf%d" % i) for i, (first, n) in enumerate(UNITS)]
        kf_out = out_0.rearrange("b (p m) h w -> p (b m) (h w)", m=HALVES)
        pairs = keep.tile([P, N // 2, HALVES], F32, name="pairs")
        sums = keep.tile([P, HALVES, TOKENS], F32, name="sums")
        unit_sums = keep.tile([P, HALVES, N_UNITS], F32, name="unit_sums")
        val_t = keep.tile([P, N_UNITS, CV], F32, name="val_t")
        key_bank = {}
        val_bank = {}

        def regroup(i, g, copy):
            first, n = UNITS[i]
            load = LOAD_OF[i]
            here = raw[load][:, g, :, first - LOADS[load][0] : first - LOADS[load][0] + n]
            if n == P:
                copy(
                    out=grouped[i][:, g].rearrange("p (j r) t -> p j t r", r=4),
                    in_=here.rearrange("p t (j r) -> p j t r", r=4),
                )
            else:
                copy(
                    out=grouped[i][:, g].rearrange("p (e j r) t -> p e j t r", e=2, r=4),
                    in_=here.rearrange("p t (j r e) -> p e j t r", e=2, r=4),
                )

        def quantise(i):
            nc.vector.quantize_mx(
                out=x_codes[i][:].rearrange("p g n -> p (g n)").bitcast(FP8X4),
                scales=x_scales[i][:].rearrange("p g n -> p (g n)"),
                in_=grouped[i][:].rearrange("p g n t -> p (g n t)"),
            )

        def project_keys(i):
            first, n = UNITS[i]
            key_bank[i] = key_banks.tile([P, HALVES, BANK // HALVES], F32, name="key_bank", tag="keys")
            for m in range(HALVES):
                for g in range(PASSES):
                    nc.tensor.matmul_mx(
                        out=key_bank[i][:, m, 0:n],
                        lhsT=wk_codes[:, g, m * P : (m + 1) * P].bitcast(FP8X4),
                        lhsT_scale=wk_scales[:, g, m * P : (m + 1) * P],
                        rhs=x_codes[i][:, g, :].bitcast(FP8X4),
                        rhs_scale=x_scales[i][:, g, :],
                        start=(g == 0),
                        stop=(g == PASSES - 1),
                    )

        def project_values(i):
            first, n = UNITS[i]
            val_bank[i] = val_banks.tile([P, BANK], F32, name="val_bank", tag="vals")
            steps = [(e, g) for e in range(n // P) for g in range(PASSES)]
            for e, g in steps:
                nc.tensor.matmul_mx(
                    out=val_bank[i][:, 0:CV],
                    lhsT=x_codes[i][:, g, e * P : (e + 1) * P].bitcast(FP8X4),
                    lhsT_scale=x_scales[i][:, g, e * P : (e + 1) * P],
                    rhs=wv_codes[:, g, :].bitcast(FP8X4),
                    rhs_scale=wv_scales[:, g, :],
                    start=((e, g) == steps[0]),
                    stop=((e, g) == steps[-1]),
                )

        def leave_values(i):
            nc.scalar.copy(out=val_t[:, i, :], in_=val_bank[i][:, 0:CV])

        def leave_keys(i):
            first, n = UNITS[i]
            for m in range(HALVES):
                out = kf[i][:, m, :]
                in_ = key_bank[i][:, m, 0:n]
                if n > P:
                    out = out.rearrange("p (j e) -> p j e", e=2)
                    in_ = in_.rearrange("p (e j) -> p j e", e=2)
                nc.scalar.activation(
                    out=out,
                    in_=in_,
                    func=ACT.Relu,
                    bias=shift[:, m : m + 1],
                    scale=scale[:, m : m + 1],
                    accum_out=unit_sums[:, m, i : i + 1],
                )
            nc.sync.dma_start(out=kf_out[:, :, first : first + n], in_=kf[i][:])

        def begin_values():
            nc.tensor.matmul(out=value_sum[:, 0:CV], lhsT=bias_pick[:], rhs=bv_row[:], start=True, stop=False)

        def pool_values(i):
            nc.tensor.matmul(
                out=value_sum[:, 0:CV], lhsT=pool[:, i, :], rhs=val_t[:, i, :], start=False, stop=(i == N_UNITS - 1)
            )

        def pair_keys(i):
            first, n = UNITS[i]
            two = kf[i][:].rearrange("p m (q e) -> p q e m", e=2)
            adder = nc.gpsimd if i < 2 else nc.vector
            adder.tensor_tensor(
                out=pairs[:, first // 2 : (first + n) // 2, :], in0=two[:, :, 0, :], in1=two[:, :, 1, :], op=ALU.add
            )

        def pool_keys(i):
            for s, b0, b1 in BANDS_AFTER[i]:
                pool_bands(s, b0, b1)

        def pool_bands(s, b0, b1):
            half_band = H // s * W // 2
            out = sums[:, :, FIRST[s] + b0 * s : FIRST[s] + b1 * s]
            in_ = pairs[:, b0 * half_band : b1 * half_band, :]
            if b1 - b0 == 1:
                nc.vector.tensor_reduce(
                    out=out, in_=in_.rearrange("p (r c x) m -> p m c r x", r=H // s, c=s), axis=AXIS.XY, op=ALU.add
                )
            else:
                for m in range(HALVES):
                    nc.vector.tensor_reduce(
                        out=out[:, m, :].rearrange("p (b c) -> p b c", c=s),
                        in_=in_[:, :, m].rearrange("p (b r c x) -> p b c r x", b=b1 - b0, r=H // s, c=s),
                        axis=AXIS.XY,
                        op=ALU.add,
                    )

        def pool_thirds(h):
            nc.vector.tensor_reduce(
                out=sums[:, :, FIRST[3] + 3 * h : FIRST[3] + 3 * (h + 1)],
                in_=sums[:, :, FIRST[6] + 12 * h : FIRST[6] + 12 * (h + 1)].rearrange(
                    "p m (b c x) -> p m c b x", b=2, x=2
                ),
                axis=AXIS.XY,
                op=ALU.add,
            )

        on_vector = nc.vector.tensor_copy
        on_scalar = nc.scalar.copy

        def keep_awake(times):
            for i in range(times):
                nc.tensor.matmul(out=value_sum[:, 0:P], lhsT=ident[:], rhs=ident[:], start=True, stop=True)

        def keep_awake_by_codes(times):
            for i in range(times):
                nc.tensor.matmul_mx(
                    out=value_sum[:, 0:CK],
                    lhsT=wk_codes[:, 0, 0:P].bitcast(FP8X4),
                    lhsT_scale=wk_scales[:, 0, 0:P],
                    rhs=wk_codes[:, 0, :].bitcast(FP8X4),
                    rhs_scale=wk_scales[:, 0, :],
                    start=True,
                    stop=True,
                )

        keep_awake(3)
        flips = [flip_weight(wk_rows, r, key_banks, "keys") for r in range(HALVES)]
        keep_awake(4)
        group_weight(wk_grouped, flips[0], 0, on_vector)
        regroup(0, 0, on_vector)
        group_weight(wk_grouped, flips[1], 1, on_scalar)
        regroup(1, 0, on_scalar)
        wk_codes, wk_scales = quantise_weight(wk_grouped, "wk")
        keep_awake_by_codes(5)
        regroup(0, 1, on_vector)
        regroup(1, 1, on_scalar)
        quantise(0)
        flips = [flip_weight(wv_rows, r, val_banks, "vals") for r in range(HALVES)]
        group_weight(wv_grouped, flips[0], 0, on_scalar)
        group_weight(wv_grouped, flips[1], 1, on_scalar)
        quantise(1)
        project_keys(0)
        project_keys(1)
        regroup(2, 0, on_vector)
        token_weight = keep.tile([P, 1], F32, name="token_weight")
        diagonal = keep.tile([P, TOKENS], F32, name="diagonal")
        nc.vector.scalar_tensor_tensor(
            out=diagonal[:],
            in0=ident[:, 0:TOKENS],
            scalar=1.0,
            in1=weight[:],
            op0=ALU.mult,
            op1=ALU.mult,
            accum_out=token_weight[:],
        )
        wv_codes, wv_scales = quantise_weight(wv_grouped, "wv")
        leave_keys(0)
        pair_keys(0)
        regroup(3, 0, on_scalar)
        begin_values()
        project_values(0)
        project_values(1)
        leave_values(0)
        pool_values(0)
        regroup(2, 1, on_vector)
        regroup(3, 1, on_vector)
        quantise(2)
        leave_keys(1)
        pair_keys(1)
        leave_values(1)
        project_keys(2)
        project_values(2)
        pool_values(1)
        regroup(4, 0, on_vector)
        regroup(4, 1, on_vector)
        quantise(3)
        project_keys(3)
        project_values(3)
        leave_keys(2)
        quantise(4)
        leave_values(2)
        project_keys(4)
        project_values(4)
        pool_values(2)
        pool_keys(0)
        pool_keys(1)
        pair_keys(2)
        leave_keys(3)
        leave_values(3)
        pool_values(3)
        leave_keys(4)
        pool_keys(2)
        pool_thirds(0)
        pool_thirds(1)
        pair_keys(3)
        leave_values(4)
        pool_values(4)
        pool_keys(3)
        pair_keys(4)
        pool_keys(4)
        pool_thirds(2)

        value = keep.tile([P, CV], F32, name="value")
        nc.scalar.activation(out=value[:], in_=value_sum[:, 0:CV], func=ACT.Copy, scale=token_weight[:, 0:1])
        value_out = out_2.rearrange("b t c -> (b t) c")
        done = 0
        for n in (64, 32, 8, 4, 2):
            nc.scalar.dma_start(out=value_out[done : done + n, :], in_=value[done : done + n, :])
            done += n

        nc.vector.tensor_reduce(out=sums[:, :, 0:1], in_=unit_sums[:], axis=AXIS.X, op=ALU.add)
        keyp = keep.tile([P, HALVES, TOKENS], F32, name="keyp")
        nc.vector.tensor_tensor(
            out=keyp[:],
            in0=sums[:],
            in1=weight[:].unsqueeze(1).to_broadcast([P, HALVES, TOKENS]),
            op=ALU.mult,
        )
        nc.sync.dma_start(out=out_1.rearrange("b (p m) t -> p (b m) t", m=HALVES), in_=keyp[:])
